import numpy as np
import ml_dtypes


def mxq(x, axis, fmt="e4m3"):
    dtype, down = {"e4m3": (ml_dtypes.float8_e4m3fn, 7), "e5m2": (ml_dtypes.float8_e5m2, 14)}[fmt]
    v = np.moveaxis(np.asarray(x, np.float32).astype(ml_dtypes.bfloat16).astype(np.float64), axis, -1)
    blocks = v.reshape(v.shape[:-1] + (-1, 32))
    amax = np.abs(blocks).max(-1, keepdims=True)
    byte = np.maximum(np.where(amax > 0, np.frexp(amax)[1] - 1 + 127, 0) - down, 1)
    scale = np.exp2(byte - 127.0)
    codes = (blocks / scale).astype(np.float32).astype(dtype).astype(np.float64)
    return np.moveaxis((codes * scale).reshape(v.shape), -1, axis)


BF16 = ml_dtypes.bfloat16


def bf(x):
    return np.asarray(x, np.float32).astype(BF16)


def f64(x):
    return np.asarray(x).astype(np.float64)


N, D, K = 16384, 512, 128
C2 = 1.5 * np.sqrt(K)


def setup_inputs():
    centers = np.random.standard_normal((K, D)) * np.sqrt(C2 / D)
    idx = (K * np.random.random(N) ** 2).astype(np.int64)
    r = np.random.random((N, 1))
    embeds = centers[idx] + np.random.standard_normal((N, D)) * r / np.sqrt(D)
    return {"embeds": bf(embeds), "centers": bf(centers)}


def reference(embeds, centers):
    alpha = 1.0
    e, c = f64(embeds), f64(centers)
    sq = (np.sum(e * e, axis=1, keepdims=True)
          + np.sum(c * c, axis=1)[None, :]
          - 2.0 * (mxq(e, 1, "e4m3") @ mxq(c, 1, "e4m3").T))
    sq = np.maximum(sq, 0.0)
    dist = (1.0 + sq / alpha) ** (-(alpha + 1.0) / 2.0)
    q = dist / np.sum(dist, axis=1, keepdims=True)
    weight = (q * q) / np.sum(q, axis=0)
    p = weight / np.sum(weight, axis=1, keepdims=True)
    loss = np.mean(p * (np.log(p) - np.log(q)))
    return loss, q

@@ -1,0 +1,405 @@
+from contextlib import ExitStack
+
+import concourse.mybir as mybir
+from concourse.masks import make_identity
+
+FLOPS = 2 * 16384 * 512 * 128
+
+F32 = mybir.dt.float32
+BF16 = mybir.dt.bfloat16
+U32 = mybir.dt.uint32
+U8 = mybir.dt.uint8
+FP8X4 = mybir.dt.float8_e4m3fn_x4
+ALU = mybir.AluOpType
+ACT = mybir.ActivationFunctionType
+
+P = 128
+N_ROWS = 16384
+D = 512
+K = 128
+TPC = 8
+CHUNK = TPC * P
+NCH = N_ROWS // CHUNK
+E_BUFS = 4
+LN_LAG = 3
+ROW_SUMS_ON_VECTOR = ()
+SCALE_ON_SCALAR = (0, 1, 3, 4, 5, 6, 8, 9, 10, 11, 13, 14, 15)
+
+
+def tile_dec_kernel(tc, embeds, centers, out_0, out_1):
+    nc = tc.nc
+    with ExitStack() as ctx:
+        const = ctx.enter_context(tc.tile_pool(name="const", bufs=1))
+        keep = ctx.enter_context(tc.tile_pool(name="keep", bufs=1))
+        stream = ctx.enter_context(tc.tile_pool(name="stream", bufs=2))
+        psum = ctx.enter_context(tc.psum_pool(name="psum", bufs=1))
+        ctx.enter_context(tc.manual_schedule())
+
+        ident = const.tile([P, P], F32, name="ident")
+        make_identity(nc, ident[:])
+        ones = const.tile([P, P], F32, name="ones")
+        nc.vector.memset(ones[:], 1.0)
+        warm = const.tile([P, 1], F32, name="warm")
+        nc.scalar.activation(out=warm[:], in_=ones[:, 0:1], func=ACT.Ln)
+
+        e2 = const.tile([P, P], F32, name="e2")
+
+        e2g = const.tile([P, NCH], F32, name="e2g")
+        diag_junk = const.tile([P, P], F32, name="diag_junk")
+
+        def on_tensor(t):
+            return t % TPC == TPC - 1 and (t // TPC) % 4 != 3
+
+        def e2_of(t):
+            if on_tensor(t):
+                return e2g[:, t // TPC : t // TPC + 1]
+            return e2[:, t : t + 1]
+
+        rsum = const.tile([P, P], F32, name="rsum")
+        rrec = const.tile([P, P], F32, name="rrec")
+        ssum = const.tile([P, P], F32, name="ssum")
+        srec = const.tile([P, P], F32, name="srec")
+        sq_junk = const.tile([P, 4 * D], BF16, name="sq_junk")
+
+        c_sb = const.tile([P, D], BF16, name="c_sb")
+
+        e_tiles = {}
+
+        def load(c):
+            e_sb = stream.tile([P, TPC * D], BF16, name="e_sb%d" % c, tag="e_sb", bufs=E_BUFS)
+            src = embeds[c * CHUNK : (c + 1) * CHUNK, :].rearrange("(p j) d -> p j d", j=TPC)
+            pieces = 4 if c == 0 else 1
+            step = TPC // pieces
+            for s in range(pieces):
+                nc.sync.dma_start(
+                    out=e_sb[:, s * step * D : (s + 1) * step * D],
+                    in_=src[:, s * step : (s + 1) * step, :].rearrange("p j d -> p (j d)"),
+                )
+            e_tiles[c] = e_sb
+
+        load(0)
+        nc.sync.dma_start(out=c_sb[:], in_=centers)
+        for c in range(1, E_BUFS):
+            load(c)
+
+        c2col = const.tile([P, 1], F32, name="c2col")
+        c_grp = const.tile([P, 4 * K], BF16, name="c_grp", align_bytes=64)
+        c_codes = const.tile([P, K], U32, name="c_codes", align_bytes=64)
+        c_scl = const.tile([P, K], U8, name="c_scl", align_bytes=64)
+        c2p1 = const.tile([P, K], F32, name="c2p1")
+
+        def centre_prep():
+            nc.scalar.activation(out=sq_junk[:, 0:D], in_=c_sb[:], func=ACT.Square, accum_out=c2col[:])
+            xtc = psum.tile([P, 2 * P], F32, name="xtc", tag="m2")
+            c_words = c_sb[:].bitcast(F32)
+            for u in range(2):
+                nc.tensor.transpose(xtc[:, u * P : (u + 1) * P], c_words[:, u * P : (u + 1) * P], ident[:])
+            nc.vector.tensor_copy(
+                out=c_grp[:].bitcast(F32).rearrange("p (r u) -> p r u", u=2),
+                in_=xtc[:].rearrange("p (u r) -> p r u", u=2),
+            )
+            c2ps = psum.tile([P, K], F32, name="c2ps", tag="m3")
+            nc.tensor.transpose(c2ps[:], c2col[:, 0:1].to_broadcast([P, P]), ident[:])
+            nc.vector.tensor_scalar_add(out=c2p1[:], in0=c2ps[:], scalar1=1.0)
+            nc.vector.quantize_mx(out=c_codes[:].bitcast(FP8X4), scales=c_scl[:], in_=c_grp[:])
+
+        l_tiles = {}
+        grp_tiles = {}
+        code_tiles = {}
+        prod_tiles = {}
+
+        def transposes(c):
+            words = e_tiles[c][:].bitcast(F32)
+            banks = []
+            for b in range(4):
+                xt = psum.tile([P, 4 * P], F32, name="xt%d_%d" % (c, b), tag="t%d" % b)
+                for s in range(4):
+                    col = (b * 4 + s) * P
+                    nc.tensor.transpose(xt[:, s * P : (s + 1) * P], words[:, col : col + P], ident[:])
+                banks.append(xt)
+            return banks
+
+        def squares(c):
+            for j in range(TPC):
+                if not on_tensor(c * TPC + j):
+                    nc.scalar.activation(
+                        out=sq_junk[:, (j % 4) * D : (j % 4 + 1) * D],
+                        in_=e_tiles[c][:, j * D : (j + 1) * D],
+                        func=ACT.Square,
+                        accum_out=e2[:, c * TPC + j : c * TPC + j + 1],
+                    )
+
+        gram_tiles = {}
+
+        def gram(c):
+            j = TPC - 1
+            if on_tensor(c * TPC + j):
+                g_ps = psum.tile([P, P], F32, name="gram%d" % c, tag="m%d" % (2 * (c % 2)))
+                view = grp_tiles[c][:].rearrange("p (j r t) -> p j r t", j=TPC, t=4)
+                for t in range(4):
+                    nc.tensor.matmul(
+                        out=g_ps[:], lhsT=view[:, j, :, t], rhs=view[:, j, :, t], start=(t == 0), stop=(t == 3)
+                    )
+                gram_tiles[c] = g_ps
+
+        def diagonal(c):
+            if c in gram_tiles:
+                nc.vector.scalar_tensor_tensor(
+                    out=diag_junk[:],
+                    in0=gram_tiles[c][:],
+                    scalar=1.0,
+                    in1=ident[:],
+                    op0=ALU.mult,
+                    op1=ALU.mult,
+                    accum_out=e2g[:, c : c + 1],
+                )
+
+        def copies(c, banks):
+            grp = stream.tile([P, TPC * D], BF16, name="grp%d" % c, tag="grp", align_bytes=64)
+            grp_words = grp[:].bitcast(F32)
+            for b in range(4):
+                nc.vector.tensor_copy(
+                    out=grp_words[:, b * 512 : (b + 1) * 512].rearrange("p (j r u) -> p j r u", j=2, u=2),
+                    in_=banks[b][:].rearrange("p (j u r) -> p j r u", j=2, u=2),
+                )
+            grp_tiles[c] = grp
+
+        def quantise(c):
+            codes = stream.tile([P, TPC * P], U32, name="codes%d" % c, tag="codes", align_bytes=64)
+            scl = stream.tile([P, TPC * P], U8, name="scl%d" % c, tag="scl", align_bytes=64)
+            nc.vector.quantize_mx(out=codes[:].bitcast(FP8X4), scales=scl[:], in_=grp_tiles[c][:])
+            code_tiles[c] = (codes, scl)
+
+        def products(c):
+            codes, scl = code_tiles[c]
+            prods = []
+            for h in range(2):
+                prod = psum.tile([P, 4 * K], F32, name="prod%d_%d" % (c, h), tag="m%d" % (2 * (c % 2) + h))
+                for s in range(4):
+                    j = h * 4 + s
+                    nc.tensor.matmul_mx(
+                        out=prod[:, s * K : (s + 1) * K],
+                        lhsT=codes[:, j * P : (j + 1) * P].bitcast(FP8X4),
+                        lhsT_scale=scl[:, j * P : (j + 1) * P],
+                        rhs=c_codes[:].bitcast(FP8X4),
+                        rhs_scale=c_scl[:],
+                        start=True,
+                        stop=True,
+                    )
+                prods.append(prod)
+            prod_tiles[c] = prods
+
+        def distances(c):
+            lt = keep.tile([P, TPC * K], F32, name="lt%d" % c, tag="lt%d" % c)
+            for h in range(2):
+                nc.vector.scalar_tensor_tensor(
+                    out=lt[:, h * 512 : (h + 1) * 512].rearrange("p (j k) -> p j k", j=4),
+                    in0=prod_tiles[c][h][:].rearrange("p (j k) -> p j k", j=4),
+                    scalar=-2.0,
+                    in1=c2p1[:].unsqueeze(1).to_broadcast([P, 4, K]),
+                    op0=ALU.mult,
+                    op1=ALU.add,
+                )
+            for j in range(TPC):
+                t = c * TPC + j
+                nc.vector.tensor_scalar(
+                    out=lt[:, j * K : (j + 1) * K],
+                    in0=lt[:, j * K : (j + 1) * K],
+                    scalar1=e2_of(t),
+                    scalar2=1.0,
+                    op0=ALU.add,
+                    op1=ALU.max,
+                )
+            l_tiles[c] = lt
+
+        def logs(c):
+            nc.scalar.activation(out=l_tiles[c][:], in_=l_tiles[c][:], func=ACT.Ln)
+
+        for i in range(NCH + LN_LAG):
+            if i < NCH:
+                banks = transposes(i)
+            if 2 <= i <= NCH + 1:
+                products(i - 2)
+            if 1 <= i <= NCH:
+                gram(i - 1)
+            if i < NCH:
+                squares(i)
+                copies(i, banks)
+                if i == 0:
+                    centre_prep()
+                if i + E_BUFS < NCH:
+                    load(i + E_BUFS)
+            if 1 <= i <= NCH:
+                quantise(i - 1)
+                diagonal(i - 1)
+            if 2 <= i <= NCH + 1:
+                distances(i - 2)
+            if i >= LN_LAG:
+                logs(i - LN_LAG)
+
+        d_tiles = {}
+        last_tile = NCH * TPC - 1
+        facc_ps = psum.tile([P, P], F32, name="facc_ps", tag="t0")
+
+        for c in range(NCH):
+            dt_ = keep.tile([P, TPC * K], F32, name="dist%d" % c, tag="dist%d" % c)
+            d_tiles[c] = dt_
+            if c in ROW_SUMS_ON_VECTOR:
+                nc.scalar.activation(out=dt_[:], in_=l_tiles[c][:], func=ACT.Exp, scale=-1.0)
+                nc.vector.tensor_reduce(
+                    out=rsum[:, c * TPC : (c + 1) * TPC],
+                    in_=dt_[:].rearrange("p (j k) -> p j k", j=TPC),
+                    axis=mybir.AxisListType.X,
+                    op=ALU.add,
+                )
+            else:
+                for j in range(TPC):
+                    t = c * TPC + j
+                    nc.scalar.activation(
+                        out=dt_[:, j * K : (j + 1) * K],
+                        in_=l_tiles[c][:, j * K : (j + 1) * K],
+                        func=ACT.Exp,
+                        scale=-1.0,
+                        accum_out=rsum[:, t : t + 1],
+                    )
+            halves = 2 if c == NCH - 1 else 1
+            step = TPC // halves
+            for h in range(halves):
+                lo = c * TPC + h * step
+                nc.vector.reciprocal(out=rrec[:, lo : lo + step], in_=rsum[:, lo : lo + step])
+                for j in range(h * step, (h + 1) * step):
+                    t = c * TPC + j
+                    nc.vector.tensor_scalar_mul(
+                        out=dt_[:, j * K : (j + 1) * K], in0=dt_[:, j * K : (j + 1) * K], scalar1=rrec[:, t : t + 1]
+                    )
+            for j in range(TPC):
+                t = c * TPC + j
+                nc.tensor.matmul(
+                    out=facc_ps[:],
+                    lhsT=dt_[:, j * K : (j + 1) * K],
+                    rhs=ident[:],
+                    is_transpose=True,
+                    start=(t == 0),
+                    stop=(t == last_tile),
+                )
+            nc.sync.dma_start(
+                out=out_1[c * CHUNK : (c + 1) * CHUNK, :].rearrange("(p j) k -> p (j k)", j=TPC),
+                in_=dt_[:],
+            )
+
+        ln_r = const.tile([P, P], F32, name="ln_r")
+        acc_lnr = const.tile([P, 1], F32, name="acc_lnr")
+        nc.scalar.activation(out=ln_r[:], in_=rsum[:], func=ACT.Ln, accum_out=acc_lnr[:])
+        f_col = const.tile([P, 1], F32, name="f_col")
+        nc.vector.tensor_reduce(out=f_col[:], in_=facc_ps[:], axis=mybir.AxisListType.X, op=ALU.add)
+        f_ps = psum.tile([P, K], F32, name="f_ps", tag="m0")
+        nc.tensor.transpose(f_ps[:], f_col[:, 0:1].to_broadcast([P, P]), ident[:])
+        lf_b = const.tile([P, K], F32, name="lf_b")
+        nc.scalar.activation(out=lf_b[:], in_=f_ps[:], func=ACT.Ln)
+
+        accp_ps = psum.tile([P, P], F32, name="accp_ps", tag="t1")
+        ysum = const.tile([P, NCH], F32, name="ysum")
+        x_tiles = {}
+
+        def shifted(c, pieces=1):
+            step = TPC // pieces
+            for s in range(pieces):
+                part_l = l_tiles[c][:, s * step * K : (s + 1) * step * K].rearrange("p (j k) -> p j k", j=step)
+                nc.vector.scalar_tensor_tensor(
+                    out=part_l,
+                    in0=lf_b[:].unsqueeze(1).to_broadcast([P, step, K]),
+                    scalar=0.5,
+                    in1=part_l,
+                    op0=ALU.mult,
+                    op1=ALU.add,
+                )
+
+        def weights(c):
+            xt_ = stream.tile([P, TPC * K], F32, name="x%d" % c, tag="x", bufs=5)
+            x_tiles[c] = xt_
+            for j in range(TPC):
+                t = c * TPC + j
+                nc.scalar.activation(
+                    out=xt_[:, j * K : (j + 1) * K],
+                    in_=l_tiles[c][:, j * K : (j + 1) * K],
+                    func=ACT.Exp,
+                    scale=-2.0,
+                    accum_out=ssum[:, t : t + 1],
+                )
+
+        def normalise(c):
+            xd = x_tiles[c]
+            for j in range(TPC):
+                t = c * TPC + j
+                if c in SCALE_ON_SCALAR:
+                    nc.scalar.activation(
+                        out=xd[:, j * K : (j + 1) * K],
+                        in_=xd[:, j * K : (j + 1) * K],
+                        func=ACT.Copy,
+                        scale=srec[:, t : t + 1],
+                    )
+                else:
+                    nc.vector.tensor_scalar_mul(
+                        out=xd[:, j * K : (j + 1) * K], in0=xd[:, j * K : (j + 1) * K], scalar1=srec[:, t : t + 1]
+                    )
+
+        def sums(c):
+            xd = x_tiles[c]
+            yj = stream.tile([P, TPC * K], F32, name="y%d" % c, tag="y", bufs=2)
+            nc.vector.scalar_tensor_tensor(
+                out=yj[:],
+                in0=xd[:],
+                scalar=1.0,
+                in1=l_tiles[c][:],
+                op0=ALU.mult,
+                op1=ALU.mult,
+                accum_out=ysum[:, c : c + 1],
+            )
+            for j in range(TPC):
+                t = c * TPC + j
+                nc.tensor.matmul(
+                    out=accp_ps[:],
+                    lhsT=xd[:, j * K : (j + 1) * K],
+                    rhs=ident[:],
+                    is_transpose=True,
+                    start=(t == 0),
+                    stop=(t == last_tile),
+                )
+
+        shifted(0, pieces=4)
+        shifted(1)
+        for c in range(NCH + 3):
+            if c < NCH:
+                weights(c)
+            if 0 <= c - 1 < NCH:
+                d = c - 1
+                nc.vector.reciprocal(out=srec[:, d * TPC : (d + 1) * TPC], in_=ssum[:, d * TPC : (d + 1) * TPC])
+            if 0 <= c - 2 < NCH:
+                normalise(c - 2)
+            if c + 2 < NCH:
+                shifted(c + 2)
+            if 0 <= c - 3 < NCH:
+                sums(c - 3)
+
+        ln_s = const.tile([P, P], F32, name="ln_s")
+        acc_lns = const.tile([P, 1], F32, name="acc_lns")
+        nc.scalar.activation(out=ln_s[:], in_=ssum[:], func=ACT.Ln, accum_out=acc_lns[:])
+        lf_col = const.tile([P, 1], F32, name="lf_col")
+        nc.scalar.activation(out=lf_col[:], in_=f_col[:], func=ACT.Ln)
+        part = const.tile([P, 8], F32, name="part")
+        nc.vector.tensor_reduce(out=part[:, 1:2], in_=ysum[:], axis=mybir.AxisListType.X, op=ALU.add)
+        nc.vector.tensor_tensor(out=part[:, 3:4], in0=acc_lnr[:], in1=part[:, 1:2], op=ALU.subtract)
+        nc.vector.tensor_reduce(out=part[:, 0:1], in_=accp_ps[:], axis=mybir.AxisListType.X, op=ALU.add)
+        nc.vector.tensor_tensor(out=part[:, 2:3], in0=part[:, 0:1], in1=lf_col[:], op=ALU.mult)
+        nc.vector.tensor_tensor(out=part[:, 4:5], in0=part[:, 3:4], in1=acc_lns[:], op=ALU.subtract)
+        nc.vector.scalar_tensor_tensor(
+            out=part[:, 5:6], in0=part[:, 2:3], scalar=-0.5, in1=part[:, 4:5], op0=ALU.mult, op1=ALU.add
+        )
+        tot_ps = psum.tile([P, P], F32, name="tot_ps", tag="m3")
+        nc.tensor.transpose(tot_ps[:], part[:, 5:6].to_broadcast([P, P]), ident[:])
+        res = const.tile([P, 1], F32, name="res")
+        nc.scalar.activation(out=ln_s[:], in_=tot_ps[:], func=ACT.Copy, scale=1.0 / (N_ROWS * K), accum_out=res[:])
+        loss_ap = out_0
+        for extra in range(2 - len(out_0.shape)):
+            loss_ap = loss_ap.unsqueeze(0)
+        nc.sync.dma_start(out=loss_ap, in_=res[0:1, 0:1])

@@ -1,3 +1,4 @@
+import math
 from contextlib import ExitStack
 
 import concourse.mybir as mybir
@@ -20,10 +21,12 @@ K = 128
 TPC = 8
 CHUNK = TPC * P
 NCH = N_ROWS // CHUNK
-E_BUFS = 4
-LN_LAG = 3
-ROW_SUMS_ON_VECTOR = ()
-SCALE_ON_SCALAR = (0, 1, 3, 4, 5, 6, 8, 9, 10, 11, 13, 14, 15)
+HALF = TPC // 2
+E_BUFS = 5
+A_BANKS = 3
+VECTOR_SQUARES = {1: (6,), 4: (6,), 7: (6,), 10: (6,), 13: (6,)}
+SHIFT_ON_VECTOR = (2, 3, 5, 6, 8, 9, 11, 12, 14, 15)
+ROOT_HALF = math.sqrt(0.5)
 
 
 def tile_dec_kernel(tc, embeds, centers, out_0, out_1):
@@ -42,24 +45,28 @@ def tile_dec_kernel(tc, embeds, centers, out_0, out_1):
         warm = const.tile([P, 1], F32, name="warm")
         nc.scalar.activation(out=warm[:], in_=ones[:, 0:1], func=ACT.Ln)
 
-        e2 = const.tile([P, P], F32, name="e2")
-
-        e2g = const.tile([P, NCH], F32, name="e2g")
+        e2h = const.tile([P, P], F32, name="e2h")
+        e2v = const.tile([P, P], F32, name="e2v")
         diag_junk = const.tile([P, P], F32, name="diag_junk")
 
         def on_tensor(t):
             return t % TPC == TPC - 1 and (t // TPC) % 4 != 3
 
-        def e2_of(t):
-            if on_tensor(t):
-                return e2g[:, t // TPC : t // TPC + 1]
-            return e2[:, t : t + 1]
+        def on_vector(t):
+            return t % TPC in VECTOR_SQUARES.get(t // TPC, ())
+
+        def e2h_of(t):
+            if on_tensor(t) or on_vector(t):
+                return e2v[:, t : t + 1]
+            return e2h[:, t : t + 1]
 
         rsum = const.tile([P, P], F32, name="rsum")
         rrec = const.tile([P, P], F32, name="rrec")
         ssum = const.tile([P, P], F32, name="ssum")
         srec = const.tile([P, P], F32, name="srec")
+        tsum = const.tile([P, P], F32, name="tsum")
         sq_junk = const.tile([P, 4 * D], BF16, name="sq_junk")
+        v_junk = const.tile([P, D], BF16, name="v_junk")
 
         c_sb = const.tile([P, D], BF16, name="c_sb")
 
@@ -82,15 +89,18 @@ def tile_dec_kernel(tc, embeds, centers, out_0, out_1):
         for c in range(1, E_BUFS):
             load(c)
 
-        c2col = const.tile([P, 1], F32, name="c2col")
+        c2h_col = const.tile([P, 1], F32, name="c2h_col")
+        c2p1_col = const.tile([P, 1], F32, name="c2p1_col")
         c_grp = const.tile([P, 4 * K], BF16, name="c_grp", align_bytes=64)
         c_codes = const.tile([P, K], U32, name="c_codes", align_bytes=64)
         c_scl = const.tile([P, K], U8, name="c_scl", align_bytes=64)
-        c2p1 = const.tile([P, K], F32, name="c2p1")
+        c2h_row = const.tile([P, K], F32, name="c2h_row")
 
         def centre_prep():
-            nc.scalar.activation(out=sq_junk[:, 0:D], in_=c_sb[:], func=ACT.Square, accum_out=c2col[:])
-            xtc = psum.tile([P, 2 * P], F32, name="xtc", tag="m2")
+            nc.scalar.activation(
+                out=sq_junk[:, 0:D], in_=c_sb[:], func=ACT.Square, scale=ROOT_HALF, accum_out=c2h_col[:]
+            )
+            xtc = psum.tile([P, 2 * P], F32, name="xtc", tag="m0")
             c_words = c_sb[:].bitcast(F32)
             for u in range(2):
                 nc.tensor.transpose(xtc[:, u * P : (u + 1) * P], c_words[:, u * P : (u + 1) * P], ident[:])
@@ -98,43 +108,56 @@ def tile_dec_kernel(tc, embeds, centers, out_0, out_1):
                 out=c_grp[:].bitcast(F32).rearrange("p (r u) -> p r u", u=2),
                 in_=xtc[:].rearrange("p (u r) -> p r u", u=2),
             )
-            c2ps = psum.tile([P, K], F32, name="c2ps", tag="m3")
-            nc.tensor.transpose(c2ps[:], c2col[:, 0:1].to_broadcast([P, P]), ident[:])
-            nc.vector.tensor_scalar_add(out=c2p1[:], in0=c2ps[:], scalar1=1.0)
+            c2ps = psum.tile([P, K], F32, name="c2ps", tag="m1")
+            nc.tensor.transpose(c2ps[:], c2h_col[:, 0:1].to_broadcast([P, P]), ident[:])
+            nc.vector.tensor_copy(out=c2h_row[:], in_=c2ps[:])
+            nc.vector.tensor_scalar(
+                out=c2p1_col[:], in0=c2h_col[:], scalar1=2.0, scalar2=1.0, op0=ALU.mult, op1=ALU.add
+            )
             nc.vector.quantize_mx(out=c_codes[:].bitcast(FP8X4), scales=c_scl[:], in_=c_grp[:])
 
-        l_tiles = {}
         grp_tiles = {}
         code_tiles = {}
         prod_tiles = {}
+        u_tiles = {}
+        l_tiles = {}
+        gram_tiles = {}
 
         def transposes(c):
             words = e_tiles[c][:].bitcast(F32)
             banks = []
             for b in range(4):
-                xt = psum.tile([P, 4 * P], F32, name="xt%d_%d" % (c, b), tag="t%d" % b)
+                xt = psum.tile([P, 4 * P], F32, name="xt%d_%d" % (c, b), tag="t%d" % ((4 * c + b) % A_BANKS))
                 for s in range(4):
                     col = (b * 4 + s) * P
                     nc.tensor.transpose(xt[:, s * P : (s + 1) * P], words[:, col : col + P], ident[:])
                 banks.append(xt)
             return banks
 
-        def squares(c):
-            for j in range(TPC):
-                if not on_tensor(c * TPC + j):
+        def squares(c, tiles):
+            for j in tiles:
+                t = c * TPC + j
+                if not on_tensor(t) and not on_vector(t):
                     nc.scalar.activation(
                         out=sq_junk[:, (j % 4) * D : (j % 4 + 1) * D],
                         in_=e_tiles[c][:, j * D : (j + 1) * D],
                         func=ACT.Square,
-                        accum_out=e2[:, c * TPC + j : c * TPC + j + 1],
+                        scale=ROOT_HALF,
+                        accum_out=e2h[:, t : t + 1],
                     )
 
-        gram_tiles = {}
+        def squares_on_vector(c):
+            for j in VECTOR_SQUARES.get(c, ()):
+                t = c * TPC + j
+                part = e_tiles[c][:, j * D : (j + 1) * D]
+                nc.vector.scalar_tensor_tensor(
+                    out=v_junk[:], in0=part, scalar=0.5, in1=part, op0=ALU.mult, op1=ALU.mult, accum_out=e2v[:, t : t + 1]
+                )
 
         def gram(c):
             j = TPC - 1
             if on_tensor(c * TPC + j):
-                g_ps = psum.tile([P, P], F32, name="gram%d" % c, tag="m%d" % (2 * (c % 2)))
+                g_ps = psum.tile([P, P], F32, name="gram%d" % c, tag="g")
                 view = grp_tiles[c][:].rearrange("p (j r t) -> p j r t", j=TPC, t=4)
                 for t in range(4):
                     nc.tensor.matmul(
@@ -144,14 +167,15 @@ def tile_dec_kernel(tc, embeds, centers, out_0, out_1):
 
         def diagonal(c):
             if c in gram_tiles:
+                t = c * TPC + TPC - 1
                 nc.vector.scalar_tensor_tensor(
                     out=diag_junk[:],
                     in0=gram_tiles[c][:],
-                    scalar=1.0,
+                    scalar=0.5,
                     in1=ident[:],
                     op0=ALU.mult,
                     op1=ALU.mult,
-                    accum_out=e2g[:, c : c + 1],
+                    accum_out=e2v[:, t : t + 1],
                 )
 
         def copies(c, banks):
@@ -174,9 +198,9 @@ def tile_dec_kernel(tc, embeds, centers, out_0, out_1):
             codes, scl = code_tiles[c]
             prods = []
             for h in range(2):
-                prod = psum.tile([P, 4 * K], F32, name="prod%d_%d" % (c, h), tag="m%d" % (2 * (c % 2) + h))
-                for s in range(4):
-                    j = h * 4 + s
+                prod = psum.tile([P, HALF * K], F32, name="prod%d_%d" % (c, h), tag="m%d" % h)
+                for s in range(HALF):
+                    j = h * HALF + s
                     nc.tensor.matmul_mx(
                         out=prod[:, s * K : (s + 1) * K],
                         lhsT=codes[:, j * P : (j + 1) * P].bitcast(FP8X4),
@@ -189,79 +213,101 @@ def tile_dec_kernel(tc, embeds, centers, out_0, out_1):
                 prods.append(prod)
             prod_tiles[c] = prods
 
-        def distances(c):
-            lt = keep.tile([P, TPC * K], F32, name="lt%d" % c, tag="lt%d" % c)
-            for h in range(2):
-                nc.vector.scalar_tensor_tensor(
-                    out=lt[:, h * 512 : (h + 1) * 512].rearrange("p (j k) -> p j k", j=4),
-                    in0=prod_tiles[c][h][:].rearrange("p (j k) -> p j k", j=4),
-                    scalar=-2.0,
-                    in1=c2p1[:].unsqueeze(1).to_broadcast([P, 4, K]),
-                    op0=ALU.mult,
-                    op1=ALU.add,
-                )
+        def differences(c):
+            ut = stream.tile([P, TPC * K], F32, name="u%d" % c, tag="u")
             for j in range(TPC):
-                t = c * TPC + j
-                nc.vector.tensor_scalar(
-                    out=lt[:, j * K : (j + 1) * K],
-                    in0=lt[:, j * K : (j + 1) * K],
-                    scalar1=e2_of(t),
-                    scalar2=1.0,
-                    op0=ALU.add,
-                    op1=ALU.max,
+                h, s = divmod(j, HALF)
+                nc.vector.scalar_tensor_tensor(
+                    out=ut[:, j * K : (j + 1) * K],
+                    in0=prod_tiles[c][h][:, s * K : (s + 1) * K],
+                    scalar=e2h_of(c * TPC + j),
+                    in1=c2h_row[:],
+                    op0=ALU.subtract,
+                    op1=ALU.min,
                 )
-            l_tiles[c] = lt
+            u_tiles[c] = ut
 
-        def logs(c):
-            nc.scalar.activation(out=l_tiles[c][:], in_=l_tiles[c][:], func=ACT.Ln)
+        ut_banks = {}
 
-        for i in range(NCH + LN_LAG):
+        def turn(c):
+            for h in range(2):
+                bank = psum.tile([P, HALF * P], F32, name="ut%d_%d" % (c, h), tag="u%d" % h)
+                for s in range(HALF):
+                    j = h * HALF + s
+                    nc.tensor.transpose(bank[:, s * P : (s + 1) * P], u_tiles[c][:, j * K : (j + 1) * K], ident[:])
+                ut_banks[c, h] = bank
+
+        def logs(c, h):
+            if h == 0:
+                lt = keep.tile([P, TPC * P], F32, name="lt%d" % c, tag="lt%d" % c)
+                l_tiles[c] = lt
+            nc.scalar.activation(
+                out=l_tiles[c][:, h * HALF * P : (h + 1) * HALF * P],
+                in_=ut_banks[c, h][:],
+                func=ACT.Ln,
+                bias=c2p1_col[:],
+                scale=-2.0,
+            )
+
+        for i in range(NCH + 3):
             if i < NCH:
                 banks = transposes(i)
             if 2 <= i <= NCH + 1:
                 products(i - 2)
             if 1 <= i <= NCH:
                 gram(i - 1)
+            if 3 <= i:
+                turn(i - 3)
             if i < NCH:
-                squares(i)
+                squares(i, range(0, HALF))
+            if 3 <= i:
+                logs(i - 3, 0)
+            if i < NCH:
+                squares(i, range(HALF, TPC))
                 copies(i, banks)
                 if i == 0:
                     centre_prep()
                 if i + E_BUFS < NCH:
                     load(i + E_BUFS)
+            if 3 <= i:
+                logs(i - 3, 1)
             if 1 <= i <= NCH:
                 quantise(i - 1)
                 diagonal(i - 1)
+            if i < NCH:
+                squares_on_vector(i)
             if 2 <= i <= NCH + 1:
-                distances(i - 2)
-            if i >= LN_LAG:
-                logs(i - LN_LAG)
+                differences(i - 2)
 
         d_tiles = {}
         last_tile = NCH * TPC - 1
-        facc_ps = psum.tile([P, P], F32, name="facc_ps", tag="t0")
+        back_banks = {}
+        back_tags = ("t0", "t1", "t2", "m0", "m1")
 
-        for c in range(NCH):
-            dt_ = keep.tile([P, TPC * K], F32, name="dist%d" % c, tag="dist%d" % c)
+        def turn_back(c):
+            for h in range(2):
+                bank = psum.tile([P, HALF * K], F32, name="lb%d_%d" % (c, h), tag=back_tags[(2 * c + h) % len(back_tags)])
+                for s in range(HALF):
+                    j = h * HALF + s
+                    nc.tensor.transpose(bank[:, s * K : (s + 1) * K], l_tiles[c][:, j * P : (j + 1) * P], ident[:])
+                back_banks[c, h] = bank
+
+        def exps(c):
+            dt_ = stream.tile([P, TPC * K], F32, name="dist%d" % c, tag="dist", bufs=4)
             d_tiles[c] = dt_
-            if c in ROW_SUMS_ON_VECTOR:
-                nc.scalar.activation(out=dt_[:], in_=l_tiles[c][:], func=ACT.Exp, scale=-1.0)
-                nc.vector.tensor_reduce(
-                    out=rsum[:, c * TPC : (c + 1) * TPC],
-                    in_=dt_[:].rearrange("p (j k) -> p j k", j=TPC),
-                    axis=mybir.AxisListType.X,
-                    op=ALU.add,
+            for j in range(TPC):
+                t = c * TPC + j
+                h, s = divmod(j, HALF)
+                nc.scalar.activation(
+                    out=dt_[:, j * K : (j + 1) * K],
+                    in_=back_banks[c, h][:, s * K : (s + 1) * K],
+                    func=ACT.Exp,
+                    scale=-1.0,
+                    accum_out=rsum[:, t : t + 1],
                 )
-            else:
-                for j in range(TPC):
-                    t = c * TPC + j
-                    nc.scalar.activation(
-                        out=dt_[:, j * K : (j + 1) * K],
-                        in_=l_tiles[c][:, j * K : (j + 1) * K],
-                        func=ACT.Exp,
-                        scale=-1.0,
-                        accum_out=rsum[:, t : t + 1],
-                    )
+
+        def memberships(c):
+            dt_ = d_tiles[c]
             halves = 2 if c == NCH - 1 else 1
             step = TPC // halves
             for h in range(halves):
@@ -272,131 +318,135 @@ def tile_dec_kernel(tc, embeds, centers, out_0, out_1):
                     nc.vector.tensor_scalar_mul(
                         out=dt_[:, j * K : (j + 1) * K], in0=dt_[:, j * K : (j + 1) * K], scalar1=rrec[:, t : t + 1]
                     )
-            for j in range(TPC):
-                t = c * TPC + j
-                nc.tensor.matmul(
-                    out=facc_ps[:],
-                    lhsT=dt_[:, j * K : (j + 1) * K],
-                    rhs=ident[:],
-                    is_transpose=True,
-                    start=(t == 0),
-                    stop=(t == last_tile),
-                )
             nc.sync.dma_start(
                 out=out_1[c * CHUNK : (c + 1) * CHUNK, :].rearrange("(p j) k -> p (j k)", j=TPC),
                 in_=dt_[:],
             )
 
-        ln_r = const.tile([P, P], F32, name="ln_r")
-        acc_lnr = const.tile([P, 1], F32, name="acc_lnr")
-        nc.scalar.activation(out=ln_r[:], in_=rsum[:], func=ACT.Ln, accum_out=acc_lnr[:])
-        f_col = const.tile([P, 1], F32, name="f_col")
-        nc.vector.tensor_reduce(out=f_col[:], in_=facc_ps[:], axis=mybir.AxisListType.X, op=ALU.add)
-        f_ps = psum.tile([P, K], F32, name="f_ps", tag="m0")
-        nc.tensor.transpose(f_ps[:], f_col[:, 0:1].to_broadcast([P, P]), ident[:])
-        lf_b = const.tile([P, K], F32, name="lf_b")
-        nc.scalar.activation(out=lf_b[:], in_=f_ps[:], func=ACT.Ln)
+        facc_ps = psum.tile([P, P], F32, name="facc_ps", tag="g")
 
-        accp_ps = psum.tile([P, P], F32, name="accp_ps", tag="t1")
-        ysum = const.tile([P, NCH], F32, name="ysum")
-        x_tiles = {}
-
-        def shifted(c, pieces=1):
-            step = TPC // pieces
-            for s in range(pieces):
-                part_l = l_tiles[c][:, s * step * K : (s + 1) * step * K].rearrange("p (j k) -> p j k", j=step)
-                nc.vector.scalar_tensor_tensor(
-                    out=part_l,
-                    in0=lf_b[:].unsqueeze(1).to_broadcast([P, step, K]),
-                    scalar=0.5,
-                    in1=part_l,
-                    op0=ALU.mult,
-                    op1=ALU.add,
-                )
-
-        def weights(c):
-            xt_ = stream.tile([P, TPC * K], F32, name="x%d" % c, tag="x", bufs=5)
-            x_tiles[c] = xt_
-            for j in range(TPC):
-                t = c * TPC + j
-                nc.scalar.activation(
-                    out=xt_[:, j * K : (j + 1) * K],
-                    in_=l_tiles[c][:, j * K : (j + 1) * K],
-                    func=ACT.Exp,
-                    scale=-2.0,
-                    accum_out=ssum[:, t : t + 1],
-                )
-
-        def normalise(c):
-            xd = x_tiles[c]
-            for j in range(TPC):
-                t = c * TPC + j
-                if c in SCALE_ON_SCALAR:
-                    nc.scalar.activation(
-                        out=xd[:, j * K : (j + 1) * K],
-                        in_=xd[:, j * K : (j + 1) * K],
-                        func=ACT.Copy,
-                        scale=srec[:, t : t + 1],
-                    )
-                else:
-                    nc.vector.tensor_scalar_mul(
-                        out=xd[:, j * K : (j + 1) * K], in0=xd[:, j * K : (j + 1) * K], scalar1=srec[:, t : t + 1]
-                    )
-
-        def sums(c):
-            xd = x_tiles[c]
-            yj = stream.tile([P, TPC * K], F32, name="y%d" % c, tag="y", bufs=2)
-            nc.vector.scalar_tensor_tensor(
-                out=yj[:],
-                in0=xd[:],
-                scalar=1.0,
-                in1=l_tiles[c][:],
-                op0=ALU.mult,
-                op1=ALU.mult,
-                accum_out=ysum[:, c : c + 1],
-            )
+        def column_sums(c):
             for j in range(TPC):
                 t = c * TPC + j
                 nc.tensor.matmul(
-                    out=accp_ps[:],
-                    lhsT=xd[:, j * K : (j + 1) * K],
+                    out=facc_ps[:],
+                    lhsT=d_tiles[c][:, j * K : (j + 1) * K],
                     rhs=ident[:],
                     is_transpose=True,
                     start=(t == 0),
                     stop=(t == last_tile),
                 )
 
-        shifted(0, pieces=4)
-        shifted(1)
-        for c in range(NCH + 3):
-            if c < NCH:
-                weights(c)
-            if 0 <= c - 1 < NCH:
-                d = c - 1
-                nc.vector.reciprocal(out=srec[:, d * TPC : (d + 1) * TPC], in_=ssum[:, d * TPC : (d + 1) * TPC])
-            if 0 <= c - 2 < NCH:
-                normalise(c - 2)
-            if c + 2 < NCH:
-                shifted(c + 2)
-            if 0 <= c - 3 < NCH:
-                sums(c - 3)
+        for i in range(NCH + 2):
+            if i < NCH:
+                turn_back(i)
+                exps(i)
+            if 1 <= i <= NCH:
+                memberships(i - 1)
+            if 2 <= i:
+                column_sums(i - 2)
 
+        f_col = const.tile([P, 1], F32, name="f_col")
+        nc.vector.tensor_reduce(out=f_col[:], in_=facc_ps[:], axis=mybir.AxisListType.X, op=ALU.add)
+        lf_col = const.tile([P, 1], F32, name="lf_col")
+        nc.scalar.activation(out=lf_col[:], in_=f_col[:], func=ACT.Ln)
+        hlf_col = const.tile([P, 1], F32, name="hlf_col")
+        nc.vector.tensor_scalar_mul(out=hlf_col[:], in0=lf_col[:], scalar1=0.5)
+
+        x_tiles = {}
+        m_banks = {}
+        m_tags = ("t0", "t1", "m0", "m1")
+        n_tags = ("t2", "u0", "u1", "g")
+
+        def shift(c):
+            if c in SHIFT_ON_VECTOR:
+                nc.vector.tensor_scalar_add(out=l_tiles[c][:], in0=l_tiles[c][:], scalar1=hlf_col[:, 0:1])
+
+        def sum_of_turns(bank, s, tiles):
+            for n, part in enumerate(tiles):
+                nc.tensor.matmul(
+                    out=bank[:, s * K : (s + 1) * K],
+                    lhsT=part,
+                    rhs=ident[:],
+                    is_transpose=True,
+                    start=(n == 0),
+                    stop=(n == len(tiles) - 1),
+                )
+
+        def turn_shifted(c):
+            half_shift = hlf_col[:, 0:1].to_broadcast([P, P])
+            full_shift = lf_col[:, 0:1].to_broadcast([P, P])
+            for h in range(2):
+                index = (2 * c + h) % 4
+                m_bank = psum.tile([P, HALF * K], F32, name="mm%d_%d" % (c, h), tag=m_tags[index])
+                n_bank = psum.tile([P, HALF * K], F32, name="mn%d_%d" % (c, h), tag=n_tags[index])
+                for s in range(HALF):
+                    j = h * HALF + s
+                    part = l_tiles[c][:, j * P : (j + 1) * P]
+                    sum_of_turns(m_bank, s, [part] if c in SHIFT_ON_VECTOR else [part, half_shift])
+                for s in range(HALF):
+                    j = h * HALF + s
+                    part = l_tiles[c][:, j * P : (j + 1) * P]
+                    sum_of_turns(n_bank, s, [part, half_shift if c in SHIFT_ON_VECTOR else full_shift])
+                m_banks[c, h] = (m_bank, n_bank)
+
+        def weights(c):
+            xt_ = stream.tile([P, TPC * K], F32, name="x%d" % c, tag="x", bufs=3)
+            x_tiles[c] = xt_
+            for j in range(TPC):
+                t = c * TPC + j
+                h, s = divmod(j, HALF)
+                nc.scalar.activation(
+                    out=xt_[:, j * K : (j + 1) * K],
+                    in_=m_banks[c, h][0][:, s * K : (s + 1) * K],
+                    func=ACT.Exp,
+                    scale=-2.0,
+                    accum_out=ssum[:, t : t + 1],
+                )
+
+        y_junk = const.tile([P, 4 * K], F32, name="y_junk")
+
+        def sums(c):
+            for j in range(TPC):
+                t = c * TPC + j
+                h, s = divmod(j, HALF)
+                nc.vector.scalar_tensor_tensor(
+                    out=y_junk[:, s * K : (s + 1) * K],
+                    in0=m_banks[c, h][1][:, s * K : (s + 1) * K],
+                    scalar=1.0,
+                    in1=x_tiles[c][:, j * K : (j + 1) * K],
+                    op0=ALU.mult,
+                    op1=ALU.mult,
+                    accum_out=tsum[:, t : t + 1],
+                )
+            nc.vector.reciprocal(out=srec[:, c * TPC : (c + 1) * TPC], in_=ssum[:, c * TPC : (c + 1) * TPC])
+
+        shift(2)
+        for c in range(NCH + 1):
+            if c < NCH:
+                turn_shifted(c)
+                weights(c)
+            if c + 3 < NCH:
+                shift(c + 3)
+            if 1 <= c:
+                sums(c - 1)
+
+        ln_r = const.tile([P, P], F32, name="ln_r")
+        acc_lnr = const.tile([P, 1], F32, name="acc_lnr")
+        nc.scalar.activation(out=ln_r[:], in_=rsum[:], func=ACT.Ln, accum_out=acc_lnr[:])
         ln_s = const.tile([P, P], F32, name="ln_s")
         acc_lns = const.tile([P, 1], F32, name="acc_lns")
         nc.scalar.activation(out=ln_s[:], in_=ssum[:], func=ACT.Ln, accum_out=acc_lns[:])
-        lf_col = const.tile([P, 1], F32, name="lf_col")
-        nc.scalar.activation(out=lf_col[:], in_=f_col[:], func=ACT.Ln)
-        part = const.tile([P, 8], F32, name="part")
-        nc.vector.tensor_reduce(out=part[:, 1:2], in_=ysum[:], axis=mybir.AxisListType.X, op=ALU.add)
-        nc.vector.tensor_tensor(out=part[:, 3:4], in0=acc_lnr[:], in1=part[:, 1:2], op=ALU.subtract)
-        nc.vector.tensor_reduce(out=part[:, 0:1], in_=accp_ps[:], axis=mybir.AxisListType.X, op=ALU.add)
-        nc.vector.tensor_tensor(out=part[:, 2:3], in0=part[:, 0:1], in1=lf_col[:], op=ALU.mult)
-        nc.vector.tensor_tensor(out=part[:, 4:5], in0=part[:, 3:4], in1=acc_lns[:], op=ALU.subtract)
+        acc_t = const.tile([P, 1], F32, name="acc_t")
         nc.vector.scalar_tensor_tensor(
-            out=part[:, 5:6], in0=part[:, 2:3], scalar=-0.5, in1=part[:, 4:5], op0=ALU.mult, op1=ALU.add
+            out=diag_junk[:], in0=tsum[:], scalar=1.0, in1=srec[:], op0=ALU.mult, op1=ALU.mult, accum_out=acc_t[:]
         )
-        tot_ps = psum.tile([P, P], F32, name="tot_ps", tag="m3")
-        nc.tensor.transpose(tot_ps[:], part[:, 5:6].to_broadcast([P, P]), ident[:])
+        part_a = const.tile([P, 1], F32, name="part_a")
+        part_b = const.tile([P, 1], F32, name="part_b")
+        nc.vector.tensor_tensor(out=part_a[:], in0=acc_lnr[:], in1=acc_lns[:], op=ALU.subtract)
+        nc.vector.tensor_tensor(out=part_b[:], in0=part_a[:], in1=acc_t[:], op=ALU.subtract)
+        tot_ps = psum.tile([P, P], F32, name="tot_ps", tag="t0")
+        nc.tensor.transpose(tot_ps[:], part_b[:, 0:1].to_broadcast([P, P]), ident[:])
         res = const.tile([P, 1], F32, name="res")
         nc.scalar.activation(out=ln_s[:], in_=tot_ps[:], func=ACT.Copy, scale=1.0 / (N_ROWS * K), accum_out=res[:])
         loss_ap = out_0

@@ -24,8 +24,10 @@ NCH = N_ROWS // CHUNK
 HALF = TPC // 2
 E_BUFS = 5
 A_BANKS = 3
-VECTOR_SQUARES = {1: (6,), 4: (6,), 7: (6,), 10: (6,), 13: (6,)}
-SHIFT_ON_VECTOR = (2, 3, 5, 6, 8, 9, 11, 12, 14, 15)
+VECTOR_SQUARES = {c: (TPC - 2,) for c in range(NCH - 5, NCH)}
+ROW_SUMS_ON_VECTOR = range(1, 10, 2)
+SHIFT_ON_GPSIMD = tuple(range(2, NCH))
+BOTH_SHIFTS_ON_GPSIMD = tuple(range(NCH // 2, NCH))
 ROOT_HALF = math.sqrt(0.5)
 
 
@@ -198,7 +200,7 @@ def tile_dec_kernel(tc, embeds, centers, out_0, out_1):
             codes, scl = code_tiles[c]
             prods = []
             for h in range(2):
-                prod = psum.tile([P, HALF * K], F32, name="prod%d_%d" % (c, h), tag="m%d" % h)
+                prod = psum.tile([P, HALF * K], F32, name="prod%d_%d" % (c, h), tag=("t%d" % (h + 1) if c == NCH - 1 else "m%d" % h))
                 for s in range(HALF):
                     j = h * HALF + s
                     nc.tensor.matmul_mx(
@@ -214,7 +216,7 @@ def tile_dec_kernel(tc, embeds, centers, out_0, out_1):
             prod_tiles[c] = prods
 
         def differences(c):
-            ut = stream.tile([P, TPC * K], F32, name="u%d" % c, tag="u")
+            ut = stream.tile([P, TPC * K], F32, name="u%d" % c, tag="u", bufs=3)
             for j in range(TPC):
                 h, s = divmod(j, HALF)
                 nc.vector.scalar_tensor_tensor(
@@ -231,7 +233,7 @@ def tile_dec_kernel(tc, embeds, centers, out_0, out_1):
 
         def turn(c):
             for h in range(2):
-                bank = psum.tile([P, HALF * P], F32, name="ut%d_%d" % (c, h), tag="u%d" % h)
+                bank = psum.tile([P, HALF * P], F32, name="ut%d_%d" % (c, h), tag=("t%d" % ((2 * c + h) % A_BANKS) if c >= NCH - 2 else "u%d" % h))
                 for s in range(HALF):
                     j = h * HALF + s
                     nc.tensor.transpose(bank[:, s * P : (s + 1) * P], u_tiles[c][:, j * K : (j + 1) * K], ident[:])
@@ -249,33 +251,32 @@ def tile_dec_kernel(tc, embeds, centers, out_0, out_1):
                 scale=-2.0,
             )
 
-        for i in range(NCH + 3):
+        for i in range(NCH + 4):
             if i < NCH:
                 banks = transposes(i)
             if 2 <= i <= NCH + 1:
                 products(i - 2)
             if 1 <= i <= NCH:
                 gram(i - 1)
-            if 3 <= i:
-                turn(i - 3)
+            if 4 <= i:
+                turn(i - 4)
             if i < NCH:
                 squares(i, range(0, HALF))
-            if 3 <= i:
-                logs(i - 3, 0)
+            if 4 <= i:
+                logs(i - 4, 0)
             if i < NCH:
                 squares(i, range(HALF, TPC))
                 copies(i, banks)
+                squares_on_vector(i)
                 if i == 0:
                     centre_prep()
                 if i + E_BUFS < NCH:
                     load(i + E_BUFS)
-            if 3 <= i:
-                logs(i - 3, 1)
+            if 4 <= i:
+                logs(i - 4, 1)
             if 1 <= i <= NCH:
                 quantise(i - 1)
                 diagonal(i - 1)
-            if i < NCH:
-                squares_on_vector(i)
             if 2 <= i <= NCH + 1:
                 differences(i - 2)
 
@@ -293,8 +294,14 @@ def tile_dec_kernel(tc, embeds, centers, out_0, out_1):
                 back_banks[c, h] = bank
 
         def exps(c):
-            dt_ = stream.tile([P, TPC * K], F32, name="dist%d" % c, tag="dist", bufs=4)
+            dt_ = stream.tile([P, TPC * K], F32, name="dist%d" % c, tag="dist", bufs=6)
             d_tiles[c] = dt_
+            if c in ROW_SUMS_ON_VECTOR:
+                for h in range(2):
+                    nc.scalar.activation(
+                        out=dt_[:, h * HALF * K : (h + 1) * HALF * K], in_=back_banks[c, h][:], func=ACT.Exp, scale=-1.0
+                    )
+                return
             for j in range(TPC):
                 t = c * TPC + j
                 h, s = divmod(j, HALF)
@@ -308,6 +315,13 @@ def tile_dec_kernel(tc, embeds, centers, out_0, out_1):
 
         def memberships(c):
             dt_ = d_tiles[c]
+            if c in ROW_SUMS_ON_VECTOR:
+                nc.vector.tensor_reduce(
+                    out=rsum[:, c * TPC : (c + 1) * TPC],
+                    in_=dt_[:].rearrange("p (j k) -> p j k", j=TPC),
+                    axis=mybir.AxisListType.X,
+                    op=ALU.add,
+                )
             halves = 2 if c == NCH - 1 else 1
             step = TPC // halves
             for h in range(halves):
@@ -337,30 +351,46 @@ def tile_dec_kernel(tc, embeds, centers, out_0, out_1):
                     stop=(t == last_tile),
                 )
 
+        turn_back(0)
         for i in range(NCH + 2):
+            if i + 1 < NCH:
+                turn_back(i + 1)
             if i < NCH:
-                turn_back(i)
                 exps(i)
             if 1 <= i <= NCH:
                 memberships(i - 1)
             if 2 <= i:
                 column_sums(i - 2)
 
+        ln_r = const.tile([P, P], F32, name="ln_r")
+        acc_lnr = const.tile([P, 1], F32, name="acc_lnr")
+        nc.scalar.activation(out=ln_r[:], in_=rsum[:], func=ACT.Ln, accum_out=acc_lnr[:])
         f_col = const.tile([P, 1], F32, name="f_col")
         nc.vector.tensor_reduce(out=f_col[:], in_=facc_ps[:], axis=mybir.AxisListType.X, op=ALU.add)
         lf_col = const.tile([P, 1], F32, name="lf_col")
         nc.scalar.activation(out=lf_col[:], in_=f_col[:], func=ACT.Ln)
-        hlf_col = const.tile([P, 1], F32, name="hlf_col")
-        nc.vector.tensor_scalar_mul(out=hlf_col[:], in0=lf_col[:], scalar1=0.5)
+        hlf = const.tile([P, P], F32, name="hlf")
+        nc.vector.tensor_scalar_mul(out=hlf[:], in0=lf_col[:, 0:1].to_broadcast([P, P]), scalar1=0.5)
+        lf = const.tile([P, P], F32, name="lf")
+        nc.vector.tensor_copy(out=lf[:], in_=lf_col[:, 0:1].to_broadcast([P, P]))
 
         x_tiles = {}
         m_banks = {}
+        shifted_tiles = {}
         m_tags = ("t0", "t1", "m0", "m1")
         n_tags = ("t2", "u0", "u1", "g")
 
         def shift(c):
-            if c in SHIFT_ON_VECTOR:
-                nc.vector.tensor_scalar_add(out=l_tiles[c][:], in0=l_tiles[c][:], scalar1=hlf_col[:, 0:1])
+            if c in SHIFT_ON_GPSIMD:
+                st = stream.tile([P, TPC * P], F32, name="shifted%d" % c, tag="shifted", bufs=4)
+                nc.gpsimd.tensor_scalar(
+                    out=st[:], in0=l_tiles[c][:], scalar1=1.0, scalar2=lf_col[:, 0:1], op0=ALU.mult, op1=ALU.add
+                )
+                shifted_tiles[c] = st
+            if c in BOTH_SHIFTS_ON_GPSIMD:
+                nc.gpsimd.tensor_scalar(
+                    out=l_tiles[c][:], in0=l_tiles[c][:], scalar1=1.0, scalar2=hlf[:, 0:1], op0=ALU.mult, op1=ALU.add
+                )
 
         def sum_of_turns(bank, s, tiles):
             for n, part in enumerate(tiles):
@@ -374,20 +404,18 @@ def tile_dec_kernel(tc, embeds, centers, out_0, out_1):
                 )
 
         def turn_shifted(c):
-            half_shift = hlf_col[:, 0:1].to_broadcast([P, P])
-            full_shift = lf_col[:, 0:1].to_broadcast([P, P])
             for h in range(2):
                 index = (2 * c + h) % 4
                 m_bank = psum.tile([P, HALF * K], F32, name="mm%d_%d" % (c, h), tag=m_tags[index])
                 n_bank = psum.tile([P, HALF * K], F32, name="mn%d_%d" % (c, h), tag=n_tags[index])
                 for s in range(HALF):
-                    j = h * HALF + s
-                    part = l_tiles[c][:, j * P : (j + 1) * P]
-                    sum_of_turns(m_bank, s, [part] if c in SHIFT_ON_VECTOR else [part, half_shift])
+                    cols = slice((h * HALF + s) * P, (h * HALF + s + 1) * P)
+                    sum_of_turns(m_bank, s, [l_tiles[c][:, cols]] if c in BOTH_SHIFTS_ON_GPSIMD else [l_tiles[c][:, cols], hlf[:]])
                 for s in range(HALF):
-                    j = h * HALF + s
-                    part = l_tiles[c][:, j * P : (j + 1) * P]
-                    sum_of_turns(n_bank, s, [part, half_shift if c in SHIFT_ON_VECTOR else full_shift])
+                    cols = slice((h * HALF + s) * P, (h * HALF + s + 1) * P)
+                    sum_of_turns(
+                        n_bank, s, [shifted_tiles[c][:, cols]] if c in SHIFT_ON_GPSIMD else [l_tiles[c][:, cols], lf[:]]
+                    )
                 m_banks[c, h] = (m_bank, n_bank)
 
         def weights(c):
@@ -422,18 +450,16 @@ def tile_dec_kernel(tc, embeds, centers, out_0, out_1):
             nc.vector.reciprocal(out=srec[:, c * TPC : (c + 1) * TPC], in_=ssum[:, c * TPC : (c + 1) * TPC])
 
         shift(2)
+        shift(3)
         for c in range(NCH + 1):
             if c < NCH:
                 turn_shifted(c)
                 weights(c)
-            if c + 3 < NCH:
-                shift(c + 3)
+            if c + 4 < NCH:
+                shift(c + 4)
             if 1 <= c:
                 sums(c - 1)
 
-        ln_r = const.tile([P, P], F32, name="ln_r")
-        acc_lnr = const.tile([P, 1], F32, name="acc_lnr")
-        nc.scalar.activation(out=ln_r[:], in_=rsum[:], func=ACT.Ln, accum_out=acc_lnr[:])
         ln_s = const.tile([P, P], F32, name="ln_s")
         acc_lns = const.tile([P, 1], F32, name="acc_lns")
         nc.scalar.activation(out=ln_s[:], in_=ssum[:], func=ACT.Ln, accum_out=acc_lns[:])

@@ -24,10 +24,11 @@ NCH = N_ROWS // CHUNK
 HALF = TPC // 2
 E_BUFS = 5
 A_BANKS = 3
-VECTOR_SQUARES = {c: (TPC - 2,) for c in range(NCH - 5, NCH)}
 ROW_SUMS_ON_VECTOR = range(1, 10, 2)
-SHIFT_ON_GPSIMD = tuple(range(2, NCH))
-BOTH_SHIFTS_ON_GPSIMD = tuple(range(NCH // 2, NCH))
+SHIFTS_ON_VECTOR = 2
+BOTH_SHIFTS_ON_GPSIMD = tuple(range(4, NCH, 2))
+RECIPROCALS_AFTER = (3, 7, NCH - 3, NCH - 1)
+GPSIMD_SQUARES = NCH - 2
 ROOT_HALF = math.sqrt(0.5)
 
 
@@ -44,6 +45,10 @@ def tile_dec_kernel(tc, embeds, centers, out_0, out_1):
         make_identity(nc, ident[:])
         ones = const.tile([P, P], F32, name="ones")
         nc.vector.memset(ones[:], 1.0)
+        mean_plus = const.tile([P, P], F32, name="mean_plus")
+        nc.gpsimd.memset(mean_plus[:], 1.0 / (N_ROWS * K))
+        mean_minus = const.tile([P, P], F32, name="mean_minus")
+        nc.gpsimd.memset(mean_minus[:], -1.0 / (N_ROWS * K))
         warm = const.tile([P, 1], F32, name="warm")
         nc.scalar.activation(out=warm[:], in_=ones[:, 0:1], func=ACT.Ln)
 
@@ -54,12 +59,14 @@ def tile_dec_kernel(tc, embeds, centers, out_0, out_1):
         def on_tensor(t):
             return t % TPC == TPC - 1 and (t // TPC) % 4 != 3
 
-        def on_vector(t):
-            return t % TPC in VECTOR_SQUARES.get(t // TPC, ())
+        def on_gpsimd(t):
+            return t % TPC == TPC - 2 and t // TPC < GPSIMD_SQUARES
 
         def e2h_of(t):
-            if on_tensor(t) or on_vector(t):
+            if on_tensor(t):
                 return e2v[:, t : t + 1]
+            if on_gpsimd(t):
+                return e2p[:, t // TPC : t // TPC + 1]
             return e2h[:, t : t + 1]
 
         rsum = const.tile([P, P], F32, name="rsum")
@@ -68,7 +75,9 @@ def tile_dec_kernel(tc, embeds, centers, out_0, out_1):
         srec = const.tile([P, P], F32, name="srec")
         tsum = const.tile([P, P], F32, name="tsum")
         sq_junk = const.tile([P, 4 * D], BF16, name="sq_junk")
-        v_junk = const.tile([P, D], BF16, name="v_junk")
+        e2p = const.tile([P, NCH], F32, name="e2p")
+        sq_gp = const.tile([P, D], F32, name="sq_gp")
+        e2_gp = const.tile([P, NCH], F32, name="e2_gp")
 
         c_sb = const.tile([P, D], BF16, name="c_sb")
 
@@ -77,7 +86,7 @@ def tile_dec_kernel(tc, embeds, centers, out_0, out_1):
         def load(c):
             e_sb = stream.tile([P, TPC * D], BF16, name="e_sb%d" % c, tag="e_sb", bufs=E_BUFS)
             src = embeds[c * CHUNK : (c + 1) * CHUNK, :].rearrange("(p j) d -> p j d", j=TPC)
-            pieces = 4 if c == 0 else 1
+            pieces = {0: 8, 1: 2}.get(c, 1)
             step = TPC // pieces
             for s in range(pieces):
                 nc.sync.dma_start(
@@ -127,19 +136,23 @@ def tile_dec_kernel(tc, embeds, centers, out_0, out_1):
 
         def transposes(c):
             words = e_tiles[c][:].bitcast(F32)
-            banks = []
+            grp = stream.tile([P, TPC * D], BF16, name="grp%d" % c, tag="grp", align_bytes=64)
+            grp_words = grp[:].bitcast(F32)
             for b in range(4):
                 xt = psum.tile([P, 4 * P], F32, name="xt%d_%d" % (c, b), tag="t%d" % ((4 * c + b) % A_BANKS))
                 for s in range(4):
                     col = (b * 4 + s) * P
                     nc.tensor.transpose(xt[:, s * P : (s + 1) * P], words[:, col : col + P], ident[:])
-                banks.append(xt)
-            return banks
+                nc.vector.tensor_copy(
+                    out=grp_words[:, b * 512 : (b + 1) * 512].rearrange("p (j r u) -> p j r u", j=2, u=2),
+                    in_=xt[:].rearrange("p (j u r) -> p j r u", j=2, u=2),
+                )
+            grp_tiles[c] = grp
 
         def squares(c, tiles):
             for j in tiles:
                 t = c * TPC + j
-                if not on_tensor(t) and not on_vector(t):
+                if not on_tensor(t) and not on_gpsimd(t):
                     nc.scalar.activation(
                         out=sq_junk[:, (j % 4) * D : (j % 4 + 1) * D],
                         in_=e_tiles[c][:, j * D : (j + 1) * D],
@@ -148,13 +161,25 @@ def tile_dec_kernel(tc, embeds, centers, out_0, out_1):
                         accum_out=e2h[:, t : t + 1],
                     )
 
-        def squares_on_vector(c):
-            for j in VECTOR_SQUARES.get(c, ()):
-                t = c * TPC + j
-                part = e_tiles[c][:, j * D : (j + 1) * D]
-                nc.vector.scalar_tensor_tensor(
-                    out=v_junk[:], in0=part, scalar=0.5, in1=part, op0=ALU.mult, op1=ALU.mult, accum_out=e2v[:, t : t + 1]
+        def squares_on_gpsimd(c):
+            if c >= GPSIMD_SQUARES:
+                return
+            part = e_tiles[c][:, (TPC - 2) * D : (TPC - 1) * D]
+            nc.gpsimd.tensor_tensor(out=sq_gp[:], in0=part, in1=part, op=ALU.mult)
+            for width in (D // 2, D // 4):
+                nc.gpsimd.tensor_tensor(
+                    out=sq_gp[:, 0:width], in0=sq_gp[:, 0:width], in1=sq_gp[:, width : 2 * width], op=ALU.add
                 )
+
+        def fold(c):
+            if c >= GPSIMD_SQUARES:
+                return
+            nc.vector.tensor_reduce(
+                out=e2_gp[:, c : c + 1], in_=sq_gp[:, 0 : D // 4], axis=mybir.AxisListType.X, op=ALU.add
+            )
+            nc.gpsimd.tensor_scalar(
+                out=e2p[:, c : c + 1], in0=e2_gp[:, c : c + 1], scalar1=0.5, scalar2=0.0, op0=ALU.mult, op1=ALU.add
+            )
 
         def gram(c):
             j = TPC - 1
@@ -180,16 +205,6 @@ def tile_dec_kernel(tc, embeds, centers, out_0, out_1):
                     accum_out=e2v[:, t : t + 1],
                 )
 
-        def copies(c, banks):
-            grp = stream.tile([P, TPC * D], BF16, name="grp%d" % c, tag="grp", align_bytes=64)
-            grp_words = grp[:].bitcast(F32)
-            for b in range(4):
-                nc.vector.tensor_copy(
-                    out=grp_words[:, b * 512 : (b + 1) * 512].rearrange("p (j r u) -> p j r u", j=2, u=2),
-                    in_=banks[b][:].rearrange("p (j u r) -> p j r u", j=2, u=2),
-                )
-            grp_tiles[c] = grp
-
         def quantise(c):
             codes = stream.tile([P, TPC * P], U32, name="codes%d" % c, tag="codes", align_bytes=64)
             scl = stream.tile([P, TPC * P], U8, name="scl%d" % c, tag="scl", align_bytes=64)
@@ -200,7 +215,7 @@ def tile_dec_kernel(tc, embeds, centers, out_0, out_1):
             codes, scl = code_tiles[c]
             prods = []
             for h in range(2):
-                prod = psum.tile([P, HALF * K], F32, name="prod%d_%d" % (c, h), tag=("t%d" % (h + 1) if c == NCH - 1 else "m%d" % h))
+                prod = psum.tile([P, HALF * K], F32, name="prod%d_%d" % (c, h), tag=(("g", "m0")[h] if c == NCH - 1 else "m%d" % h))
                 for s in range(HALF):
                     j = h * HALF + s
                     nc.tensor.matmul_mx(
@@ -230,10 +245,11 @@ def tile_dec_kernel(tc, embeds, centers, out_0, out_1):
             u_tiles[c] = ut
 
         ut_banks = {}
+        late_tags = ("u0", "u1", "t0", "t1", "t2")
 
         def turn(c):
             for h in range(2):
-                bank = psum.tile([P, HALF * P], F32, name="ut%d_%d" % (c, h), tag=("t%d" % ((2 * c + h) % A_BANKS) if c >= NCH - 2 else "u%d" % h))
+                bank = psum.tile([P, HALF * P], F32, name="ut%d_%d" % (c, h), tag=(late_tags[(2 * c + h) % len(late_tags)] if c >= NCH - 4 else "u%d" % h))
                 for s in range(HALF):
                     j = h * HALF + s
                     nc.tensor.transpose(bank[:, s * P : (s + 1) * P], u_tiles[c][:, j * K : (j + 1) * K], ident[:])
@@ -252,8 +268,10 @@ def tile_dec_kernel(tc, embeds, centers, out_0, out_1):
             )
 
         for i in range(NCH + 4):
+            if i == 1:
+                quantise(0)
             if i < NCH:
-                banks = transposes(i)
+                transposes(i)
             if 2 <= i <= NCH + 1:
                 products(i - 2)
             if 1 <= i <= NCH:
@@ -266,16 +284,19 @@ def tile_dec_kernel(tc, embeds, centers, out_0, out_1):
                 logs(i - 4, 0)
             if i < NCH:
                 squares(i, range(HALF, TPC))
-                copies(i, banks)
-                squares_on_vector(i)
                 if i == 0:
                     centre_prep()
-                if i + E_BUFS < NCH:
-                    load(i + E_BUFS)
             if 4 <= i:
                 logs(i - 4, 1)
-            if 1 <= i <= NCH:
+            if 2 <= i <= NCH:
                 quantise(i - 1)
+            if 1 <= i <= NCH:
+                fold(i - 1)
+            if i < NCH:
+                squares_on_gpsimd(i)
+                if i + E_BUFS < NCH:
+                    load(i + E_BUFS)
+            if 1 <= i <= NCH:
                 diagonal(i - 1)
             if 2 <= i <= NCH + 1:
                 differences(i - 2)
@@ -371,8 +392,6 @@ def tile_dec_kernel(tc, embeds, centers, out_0, out_1):
         nc.scalar.activation(out=lf_col[:], in_=f_col[:], func=ACT.Ln)
         hlf = const.tile([P, P], F32, name="hlf")
         nc.vector.tensor_scalar_mul(out=hlf[:], in0=lf_col[:, 0:1].to_broadcast([P, P]), scalar1=0.5)
-        lf = const.tile([P, P], F32, name="lf")
-        nc.vector.tensor_copy(out=lf[:], in_=lf_col[:, 0:1].to_broadcast([P, P]))
 
         x_tiles = {}
         m_banks = {}
@@ -381,12 +400,16 @@ def tile_dec_kernel(tc, embeds, centers, out_0, out_1):
         n_tags = ("t2", "u0", "u1", "g")
 
         def shift(c):
-            if c in SHIFT_ON_GPSIMD:
-                st = stream.tile([P, TPC * P], F32, name="shifted%d" % c, tag="shifted", bufs=4)
-                nc.gpsimd.tensor_scalar(
-                    out=st[:], in0=l_tiles[c][:], scalar1=1.0, scalar2=lf_col[:, 0:1], op0=ALU.mult, op1=ALU.add
-                )
-                shifted_tiles[c] = st
+            st = stream.tile([P, TPC * P], F32, name="shifted%d" % c, tag="shifted", bufs=5)
+            shifted_tiles[c] = st
+            if c < SHIFTS_ON_VECTOR:
+                for h in range(2):
+                    cols = slice(h * HALF * P, (h + 1) * HALF * P)
+                    nc.vector.tensor_scalar_add(out=st[:, cols], in0=l_tiles[c][:, cols], scalar1=lf_col[:, 0:1])
+                return
+            nc.gpsimd.tensor_scalar(
+                out=st[:], in0=l_tiles[c][:], scalar1=1.0, scalar2=lf_col[:, 0:1], op0=ALU.mult, op1=ALU.add
+            )
             if c in BOTH_SHIFTS_ON_GPSIMD:
                 nc.gpsimd.tensor_scalar(
                     out=l_tiles[c][:], in0=l_tiles[c][:], scalar1=1.0, scalar2=hlf[:, 0:1], op0=ALU.mult, op1=ALU.add
@@ -413,9 +436,7 @@ def tile_dec_kernel(tc, embeds, centers, out_0, out_1):
                     sum_of_turns(m_bank, s, [l_tiles[c][:, cols]] if c in BOTH_SHIFTS_ON_GPSIMD else [l_tiles[c][:, cols], hlf[:]])
                 for s in range(HALF):
                     cols = slice((h * HALF + s) * P, (h * HALF + s + 1) * P)
-                    sum_of_turns(
-                        n_bank, s, [shifted_tiles[c][:, cols]] if c in SHIFT_ON_GPSIMD else [l_tiles[c][:, cols], lf[:]]
-                    )
+                    sum_of_turns(n_bank, s, [shifted_tiles[c][:, cols]])
                 m_banks[c, h] = (m_bank, n_bank)
 
         def weights(c):
@@ -447,10 +468,26 @@ def tile_dec_kernel(tc, embeds, centers, out_0, out_1):
                     op1=ALU.mult,
                     accum_out=tsum[:, t : t + 1],
                 )
-            nc.vector.reciprocal(out=srec[:, c * TPC : (c + 1) * TPC], in_=ssum[:, c * TPC : (c + 1) * TPC])
+            if c in RECIPROCALS_AFTER:
+                first = max([0] + [x + 1 for x in RECIPROCALS_AFTER if x < c])
+                cols = slice(first * TPC, (c + 1) * TPC)
+                nc.vector.reciprocal(out=srec[:, cols], in_=ssum[:, cols])
 
-        shift(2)
-        shift(3)
+        def weighted(first, last, n):
+            cols = slice(first * TPC, (last + 1) * TPC)
+            nc.vector.scalar_tensor_tensor(
+                out=diag_junk[:, cols],
+                in0=tsum[:, cols],
+                scalar=1.0,
+                in1=srec[:, cols],
+                op0=ALU.mult,
+                op1=ALU.mult,
+                accum_out=acc_t[n][:],
+            )
+
+        acc_t = [const.tile([P, 1], F32, name="acc_t%d" % n) for n in range(2)]
+        for c in range(4):
+            shift(c)
         for c in range(NCH + 1):
             if c < NCH:
                 turn_shifted(c)
@@ -458,23 +495,20 @@ def tile_dec_kernel(tc, embeds, centers, out_0, out_1):
             if c + 4 < NCH:
                 shift(c + 4)
             if 1 <= c:
+                if c == NCH:
+                    weighted(0, NCH - 3, 0)
                 sums(c - 1)
 
         ln_s = const.tile([P, P], F32, name="ln_s")
         acc_lns = const.tile([P, 1], F32, name="acc_lns")
         nc.scalar.activation(out=ln_s[:], in_=ssum[:], func=ACT.Ln, accum_out=acc_lns[:])
-        acc_t = const.tile([P, 1], F32, name="acc_t")
-        nc.vector.scalar_tensor_tensor(
-            out=diag_junk[:], in0=tsum[:], scalar=1.0, in1=srec[:], op0=ALU.mult, op1=ALU.mult, accum_out=acc_t[:]
-        )
-        part_a = const.tile([P, 1], F32, name="part_a")
-        part_b = const.tile([P, 1], F32, name="part_b")
-        nc.vector.tensor_tensor(out=part_a[:], in0=acc_lnr[:], in1=acc_lns[:], op=ALU.subtract)
-        nc.vector.tensor_tensor(out=part_b[:], in0=part_a[:], in1=acc_t[:], op=ALU.subtract)
-        tot_ps = psum.tile([P, P], F32, name="tot_ps", tag="t0")
-        nc.tensor.transpose(tot_ps[:], part_b[:, 0:1].to_broadcast([P, P]), ident[:])
+        weighted(NCH - 2, NCH - 1, 1)
+        tot_ps = psum.tile([P, 1], F32, name="tot_ps", tag="t0")
+        terms = ((mean_plus, acc_lnr), (mean_minus, acc_t[0]), (mean_minus, acc_lns), (mean_minus, acc_t[1]))
+        for n, (factor, column) in enumerate(terms):
+            nc.tensor.matmul(out=tot_ps[:], lhsT=factor[:], rhs=column[:], start=(n == 0), stop=(n == len(terms) - 1))
         res = const.tile([P, 1], F32, name="res")
-        nc.scalar.activation(out=ln_s[:], in_=tot_ps[:], func=ACT.Copy, scale=1.0 / (N_ROWS * K), accum_out=res[:])
+        nc.scalar.copy(out=res[:], in_=tot_ps[:])
         loss_ap = out_0
         for extra in range(2 - len(out_0.shape)):
             loss_ap = loss_ap.unsqueeze(0)

@@ -23,7 +23,7 @@ CHUNK = TPC * P
 NCH = N_ROWS // CHUNK
 HALF = TPC // 2
 E_BUFS = 5
-A_BANKS = 3
+A_BANKS = 4
 ROW_SUMS_ON_VECTOR = range(1, 10, 2)
 SHIFTS_ON_VECTOR = 2
 BOTH_SHIFTS_ON_GPSIMD = tuple(range(4, NCH, 2))
@@ -53,18 +53,13 @@ def tile_dec_kernel(tc, embeds, centers, out_0, out_1):
         nc.scalar.activation(out=warm[:], in_=ones[:, 0:1], func=ACT.Ln)
 
         e2h = const.tile([P, P], F32, name="e2h")
-        e2v = const.tile([P, P], F32, name="e2v")
         diag_junk = const.tile([P, P], F32, name="diag_junk")
 
-        def on_tensor(t):
-            return t % TPC == TPC - 1 and (t // TPC) % 4 != 3
 
         def on_gpsimd(t):
             return t % TPC == TPC - 2 and t // TPC < GPSIMD_SQUARES
 
         def e2h_of(t):
-            if on_tensor(t):
-                return e2v[:, t : t + 1]
             if on_gpsimd(t):
                 return e2p[:, t // TPC : t // TPC + 1]
             return e2h[:, t : t + 1]
@@ -132,7 +127,6 @@ def tile_dec_kernel(tc, embeds, centers, out_0, out_1):
         prod_tiles = {}
         u_tiles = {}
         l_tiles = {}
-        gram_tiles = {}
 
         def transposes(c):
             words = e_tiles[c][:].bitcast(F32)
@@ -152,7 +146,7 @@ def tile_dec_kernel(tc, embeds, centers, out_0, out_1):
         def squares(c, tiles):
             for j in tiles:
                 t = c * TPC + j
-                if not on_tensor(t) and not on_gpsimd(t):
+                if not on_gpsimd(t):
                     nc.scalar.activation(
                         out=sq_junk[:, (j % 4) * D : (j % 4 + 1) * D],
                         in_=e_tiles[c][:, j * D : (j + 1) * D],
@@ -181,30 +175,6 @@ def tile_dec_kernel(tc, embeds, centers, out_0, out_1):
                 out=e2p[:, c : c + 1], in0=e2_gp[:, c : c + 1], scalar1=0.5, scalar2=0.0, op0=ALU.mult, op1=ALU.add
             )
 
-        def gram(c):
-            j = TPC - 1
-            if on_tensor(c * TPC + j):
-                g_ps = psum.tile([P, P], F32, name="gram%d" % c, tag="g")
-                view = grp_tiles[c][:].rearrange("p (j r t) -> p j r t", j=TPC, t=4)
-                for t in range(4):
-                    nc.tensor.matmul(
-                        out=g_ps[:], lhsT=view[:, j, :, t], rhs=view[:, j, :, t], start=(t == 0), stop=(t == 3)
-                    )
-                gram_tiles[c] = g_ps
-
-        def diagonal(c):
-            if c in gram_tiles:
-                t = c * TPC + TPC - 1
-                nc.vector.scalar_tensor_tensor(
-                    out=diag_junk[:],
-                    in0=gram_tiles[c][:],
-                    scalar=0.5,
-                    in1=ident[:],
-                    op0=ALU.mult,
-                    op1=ALU.mult,
-                    accum_out=e2v[:, t : t + 1],
-                )
-
         def quantise(c):
             codes = stream.tile([P, TPC * P], U32, name="codes%d" % c, tag="codes", align_bytes=64)
             scl = stream.tile([P, TPC * P], U8, name="scl%d" % c, tag="scl", align_bytes=64)
@@ -215,7 +185,7 @@ def tile_dec_kernel(tc, embeds, centers, out_0, out_1):
             codes, scl = code_tiles[c]
             prods = []
             for h in range(2):
-                prod = psum.tile([P, HALF * K], F32, name="prod%d_%d" % (c, h), tag=(("g", "m0")[h] if c == NCH - 1 else "m%d" % h))
+                prod = psum.tile([P, HALF * K], F32, name="prod%d_%d" % (c, h), tag=(("t3", "m0")[h] if c == NCH - 1 else "m%d" % h))
                 for s in range(HALF):
                     j = h * HALF + s
                     nc.tensor.matmul_mx(
@@ -267,27 +237,25 @@ def tile_dec_kernel(tc, embeds, centers, out_0, out_1):
                 scale=-2.0,
             )
 
-        for i in range(NCH + 4):
+        for i in range(NCH + 3):
             if i == 1:
                 quantise(0)
             if i < NCH:
                 transposes(i)
             if 2 <= i <= NCH + 1:
                 products(i - 2)
-            if 1 <= i <= NCH:
-                gram(i - 1)
-            if 4 <= i:
-                turn(i - 4)
+            if 3 <= i:
+                turn(i - 3)
             if i < NCH:
                 squares(i, range(0, HALF))
-            if 4 <= i:
-                logs(i - 4, 0)
+            if 3 <= i:
+                logs(i - 3, 0)
             if i < NCH:
                 squares(i, range(HALF, TPC))
                 if i == 0:
                     centre_prep()
-            if 4 <= i:
-                logs(i - 4, 1)
+            if 3 <= i:
+                logs(i - 3, 1)
             if 2 <= i <= NCH:
                 quantise(i - 1)
             if 1 <= i <= NCH:
@@ -296,8 +264,6 @@ def tile_dec_kernel(tc, embeds, centers, out_0, out_1):
                 squares_on_gpsimd(i)
                 if i + E_BUFS < NCH:
                     load(i + E_BUFS)
-            if 1 <= i <= NCH:
-                diagonal(i - 1)
             if 2 <= i <= NCH + 1:
                 differences(i - 2)
 
@@ -358,7 +324,7 @@ def tile_dec_kernel(tc, embeds, centers, out_0, out_1):
                 in_=dt_[:],
             )
 
-        facc_ps = psum.tile([P, P], F32, name="facc_ps", tag="g")
+        facc_ps = psum.tile([P, P], F32, name="facc_ps", tag="t3")
 
         def column_sums(c):
             for j in range(TPC):
@@ -397,7 +363,7 @@ def tile_dec_kernel(tc, embeds, centers, out_0, out_1):
         m_banks = {}
         shifted_tiles = {}
         m_tags = ("t0", "t1", "m0", "m1")
-        n_tags = ("t2", "u0", "u1", "g")
+        n_tags = ("t2", "u0", "u1", "t3")
 
         def shift(c):
             st = stream.tile([P, TPC * P], F32, name="shifted%d" % c, tag="shifted", bufs=5)

@@ -128,11 +128,29 @@ def tile_dec_kernel(tc, embeds, centers, out_0, out_1):
         u_tiles = {}
         l_tiles = {}
 
+        spins = []
+
+        def spin(c, tag):
+            codes, scl = code_tiles[c]
+            spins.append(c)
+            bank = psum.tile([P, 4 * P], F32, name="spin%d" % len(spins), tag=tag)
+            nc.tensor.matmul_mx(
+                out=bank[:],
+                lhsT=c_codes[:].bitcast(FP8X4),
+                lhsT_scale=c_scl[:],
+                rhs=codes[:, 0 : 4 * P].bitcast(FP8X4),
+                rhs_scale=scl[:, 0 : 4 * P],
+                start=True,
+                stop=True,
+            )
+
         def transposes(c):
             words = e_tiles[c][:].bitcast(F32)
             grp = stream.tile([P, TPC * D], BF16, name="grp%d" % c, tag="grp", align_bytes=64)
             grp_words = grp[:].bitcast(F32)
             for b in range(4):
+                if b in (1, 3) and 3 <= c:
+                    spin(c - 3, "t%d" % ((4 * c + b) % A_BANKS))
                 xt = psum.tile([P, 4 * P], F32, name="xt%d_%d" % (c, b), tag="t%d" % ((4 * c + b) % A_BANKS))
                 for s in range(4):
                     col = (b * 4 + s) * P
@@ -348,6 +366,9 @@ def tile_dec_kernel(tc, embeds, centers, out_0, out_1):
                 memberships(i - 1)
             if 2 <= i:
                 column_sums(i - 2)
+
+        for n in range(3):
+            spin(NCH - 1, "u0")
 
         ln_r = const.tile([P, P], F32, name="ln_r")
         acc_lnr = const.tile([P, 1], F32, name="acc_lnr")

import math
from contextlib import ExitStack

import concourse.mybir as mybir
from concourse.masks import make_identity

FLOPS = 2 * 16384 * 512 * 128

F32 = mybir.dt.float32
BF16 = mybir.dt.bfloat16
U32 = mybir.dt.uint32
U8 = mybir.dt.uint8
FP8X4 = mybir.dt.float8_e4m3fn_x4
ALU = mybir.AluOpType
ACT = mybir.ActivationFunctionType

P = 128
N_ROWS = 16384
D = 512
K = 128
TPC = 8
CHUNK = TPC * P
NCH = N_ROWS // CHUNK
HALF = TPC // 2
E_BUFS = 5
A_BANKS = 4
ROW_SUMS_ON_VECTOR = range(1, 10, 2)
SHIFTS_ON_VECTOR = 2
BOTH_SHIFTS_ON_GPSIMD = tuple(range(4, NCH, 2))
RECIPROCALS_AFTER = (3, 7, NCH - 3, NCH - 1)
GPSIMD_SQUARES = NCH - 2
ROOT_HALF = math.sqrt(0.5)


def tile_dec_kernel(tc, embeds, centers, out_0, out_1):
    nc = tc.nc
    with ExitStack() as ctx:
        const = ctx.enter_context(tc.tile_pool(name="const", bufs=1))
        keep = ctx.enter_context(tc.tile_pool(name="keep", bufs=1))
        stream = ctx.enter_context(tc.tile_pool(name="stream", bufs=2))
        psum = ctx.enter_context(tc.psum_pool(name="psum", bufs=1))
        ctx.enter_context(tc.manual_schedule())

        ident = const.tile([P, P], F32, name="ident")
        make_identity(nc, ident[:])
        ones = const.tile([P, P], F32, name="ones")
        nc.vector.memset(ones[:], 1.0)
        mean_plus = const.tile([P, P], F32, name="mean_plus")
        nc.gpsimd.memset(mean_plus[:], 1.0 / (N_ROWS * K))
        mean_minus = const.tile([P, P], F32, name="mean_minus")
        nc.gpsimd.memset(mean_minus[:], -1.0 / (N_ROWS * K))
        warm = const.tile([P, 1], F32, name="warm")
        nc.scalar.activation(out=warm[:], in_=ones[:, 0:1], func=ACT.Ln)

        e2h = const.tile([P, P], F32, name="e2h")
        diag_junk = const.tile([P, P], F32, name="diag_junk")


        def on_gpsimd(t):
            return t % TPC == TPC - 2 and t // TPC < GPSIMD_SQUARES

        def e2h_of(t):
            if on_gpsimd(t):
                return e2p[:, t // TPC : t // TPC + 1]
            return e2h[:, t : t + 1]

        rsum = const.tile([P, P], F32, name="rsum")
        rrec = const.tile([P, P], F32, name="rrec")
        ssum = const.tile([P, P], F32, name="ssum")
        srec = const.tile([P, P], F32, name="srec")
        tsum = const.tile([P, P], F32, name="tsum")
        sq_junk = const.tile([P, 4 * D], BF16, name="sq_junk")
        e2p = const.tile([P, NCH], F32, name="e2p")
        sq_gp = const.tile([P, D], F32, name="sq_gp")
        e2_gp = const.tile([P, NCH], F32, name="e2_gp")

        c_sb = const.tile([P, D], BF16, name="c_sb")

        e_tiles = {}

        def load(c):
            e_sb = stream.tile([P, TPC * D], BF16, name="e_sb%d" % c, tag="e_sb", bufs=E_BUFS)
            src = embeds[c * CHUNK : (c + 1) * CHUNK, :].rearrange("(p j) d -> p j d", j=TPC)
            pieces = {0: 8, 1: 2}.get(c, 1)
            step = TPC // pieces
            for s in range(pieces):
                nc.sync.dma_start(
                    out=e_sb[:, s * step * D : (s + 1) * step * D],
                    in_=src[:, s * step : (s + 1) * step, :].rearrange("p j d -> p (j d)"),
                )
            e_tiles[c] = e_sb

        load(0)
        nc.sync.dma_start(out=c_sb[:], in_=centers)
        for c in range(1, E_BUFS):
            load(c)

        c2h_col = const.tile([P, 1], F32, name="c2h_col")
        c2p1_col = const.tile([P, 1], F32, name="c2p1_col")
        c_grp = const.tile([P, 4 * K], BF16, name="c_grp", align_bytes=64)
        c_codes = const.tile([P, K], U32, name="c_codes", align_bytes=64)
        c_scl = const.tile([P, K], U8, name="c_scl", align_bytes=64)
        c2h_row = const.tile([P, K], F32, name="c2h_row")

        def centre_prep():
            nc.scalar.activation(
                out=sq_junk[:, 0:D], in_=c_sb[:], func=ACT.Square, scale=ROOT_HALF, accum_out=c2h_col[:]
            )
            xtc = psum.tile([P, 2 * P], F32, name="xtc", tag="m0")
            c_words = c_sb[:].bitcast(F32)
            for u in range(2):
                nc.tensor.transpose(xtc[:, u * P : (u + 1) * P], c_words[:, u * P : (u + 1) * P], ident[:])
            nc.vector.tensor_copy(
                out=c_grp[:].bitcast(F32).rearrange("p (r u) -> p r u", u=2),
                in_=xtc[:].rearrange("p (u r) -> p r u", u=2),
            )
            c2ps = psum.tile([P, K], F32, name="c2ps", tag="m1")
            nc.tensor.transpose(c2ps[:], c2h_col[:, 0:1].to_broadcast([P, P]), ident[:])
            nc.vector.tensor_copy(out=c2h_row[:], in_=c2ps[:])
            nc.vector.tensor_scalar(
                out=c2p1_col[:], in0=c2h_col[:], scalar1=2.0, scalar2=1.0, op0=ALU.mult, op1=ALU.add
            )
            nc.vector.quantize_mx(out=c_codes[:].bitcast(FP8X4), scales=c_scl[:], in_=c_grp[:])

        grp_tiles = {}
        code_tiles = {}
        prod_tiles = {}
        u_tiles = {}
        l_tiles = {}

        spins = []

        def spin(c, tag):
            codes, scl = code_tiles[c]
            spins.append(c)
            bank = psum.tile([P, 4 * P], F32, name="spin%d" % len(spins), tag=tag)
            nc.tensor.matmul_mx(
                out=bank[:],
                lhsT=c_codes[:].bitcast(FP8X4),
                lhsT_scale=c_scl[:],
                rhs=codes[:, 0 : 4 * P].bitcast(FP8X4),
                rhs_scale=scl[:, 0 : 4 * P],
                start=True,
                stop=True,
            )

        def transposes(c):
            words = e_tiles[c][:].bitcast(F32)
            grp = stream.tile([P, TPC * D], BF16, name="grp%d" % c, tag="grp", align_bytes=64)
            grp_words = grp[:].bitcast(F32)
            for b in range(4):
                if b in (1, 3) and 3 <= c:
                    spin(c - 3, "t%d" % ((4 * c + b) % A_BANKS))
                xt = psum.tile([P, 4 * P], F32, name="xt%d_%d" % (c, b), tag="t%d" % ((4 * c + b) % A_BANKS))
                for s in range(4):
                    col = (b * 4 + s) * P
                    nc.tensor.transpose(xt[:, s * P : (s + 1) * P], words[:, col : col + P], ident[:])
                nc.vector.tensor_copy(
                    out=grp_words[:, b * 512 : (b + 1) * 512].rearrange("p (j r u) -> p j r u", j=2, u=2),
                    in_=xt[:].rearrange("p (j u r) -> p j r u", j=2, u=2),
                )
            grp_tiles[c] = grp

        def squares(c, tiles):
            for j in tiles:
                t = c * TPC + j
                if not on_gpsimd(t):
                    nc.scalar.activation(
                        out=sq_junk[:, (j % 4) * D : (j % 4 + 1) * D],
                        in_=e_tiles[c][:, j * D : (j + 1) * D],
                        func=ACT.Square,
                        scale=ROOT_HALF,
                        accum_out=e2h[:, t : t + 1],
                    )

        def squares_on_gpsimd(c):
            if c >= GPSIMD_SQUARES:
                return
            part = e_tiles[c][:, (TPC - 2) * D : (TPC - 1) * D]
            nc.gpsimd.tensor_tensor(out=sq_gp[:], in0=part, in1=part, op=ALU.mult)
            for width in (D // 2, D // 4):
                nc.gpsimd.tensor_tensor(
                    out=sq_gp[:, 0:width], in0=sq_gp[:, 0:width], in1=sq_gp[:, width : 2 * width], op=ALU.add
                )

        def fold(c):
            if c >= GPSIMD_SQUARES:
                return
            nc.vector.tensor_reduce(
                out=e2_gp[:, c : c + 1], in_=sq_gp[:, 0 : D // 4], axis=mybir.AxisListType.X, op=ALU.add
            )
            nc.gpsimd.tensor_scalar(
                out=e2p[:, c : c + 1], in0=e2_gp[:, c : c + 1], scalar1=0.5, scalar2=0.0, op0=ALU.mult, op1=ALU.add
            )

        def quantise(c):
            codes = stream.tile([P, TPC * P], U32, name="codes%d" % c, tag="codes", align_bytes=64)
            scl = stream.tile([P, TPC * P], U8, name="scl%d" % c, tag="scl", align_bytes=64)
            nc.vector.quantize_mx(out=codes[:].bitcast(FP8X4), scales=scl[:], in_=grp_tiles[c][:])
            code_tiles[c] = (codes, scl)

        def products(c):
            codes, scl = code_tiles[c]
            prods = []
            for h in range(2):
                prod = psum.tile([P, HALF * K], F32, name="prod%d_%d" % (c, h), tag=(("t3", "m0")[h] if c == NCH - 1 else "m%d" % h))
                for s in range(HALF):
                    j = h * HALF + s
                    nc.tensor.matmul_mx(
                        out=prod[:, s * K : (s + 1) * K],
                        lhsT=codes[:, j * P : (j + 1) * P].bitcast(FP8X4),
                        lhsT_scale=scl[:, j * P : (j + 1) * P],
                        rhs=c_codes[:].bitcast(FP8X4),
                        rhs_scale=c_scl[:],
                        start=True,
                        stop=True,
                    )
                prods.append(prod)
            prod_tiles[c] = prods

        def differences(c):
            ut = stream.tile([P, TPC * K], F32, name="u%d" % c, tag="u", bufs=3)
            for j in range(TPC):
                h, s = divmod(j, HALF)
                nc.vector.scalar_tensor_tensor(
                    out=ut[:, j * K : (j + 1) * K],
                    in0=prod_tiles[c][h][:, s * K : (s + 1) * K],
                    scalar=e2h_of(c * TPC + j),
                    in1=c2h_row[:],
                    op0=ALU.subtract,
                    op1=ALU.min,
                )
            u_tiles[c] = ut

        ut_banks = {}
        late_tags = ("u0", "u1", "t0", "t1", "t2")

        def turn(c):
            for h in range(2):
                bank = psum.tile([P, HALF * P], F32, name="ut%d_%d" % (c, h), tag=(late_tags[(2 * c + h) % len(late_tags)] if c >= NCH - 4 else "u%d" % h))
                for s in range(HALF):
                    j = h * HALF + s
                    nc.tensor.transpose(bank[:, s * P : (s + 1) * P], u_tiles[c][:, j * K : (j + 1) * K], ident[:])
                ut_banks[c, h] = bank

        def logs(c, h):
            if h == 0:
                lt = keep.tile([P, TPC * P], F32, name="lt%d" % c, tag="lt%d" % c)
                l_tiles[c] = lt
            nc.scalar.activation(
                out=l_tiles[c][:, h * HALF * P : (h + 1) * HALF * P],
                in_=ut_banks[c, h][:],
                func=ACT.Ln,
                bias=c2p1_col[:],
                scale=-2.0,
            )

        for i in range(NCH + 3):
            if i == 1:
                quantise(0)
            if i < NCH:
                transposes(i)
            if 2 <= i <= NCH + 1:
                products(i - 2)
            if 3 <= i:
                turn(i - 3)
            if i < NCH:
                squares(i, range(0, HALF))
            if 3 <= i:
                logs(i - 3, 0)
            if i < NCH:
                squares(i, range(HALF, TPC))
                if i == 0:
                    centre_prep()
            if 3 <= i:
                logs(i - 3, 1)
            if 2 <= i <= NCH:
                quantise(i - 1)
            if 1 <= i <= NCH:
                fold(i - 1)
            if i < NCH:
                squares_on_gpsimd(i)
                if i + E_BUFS < NCH:
                    load(i + E_BUFS)
            if 2 <= i <= NCH + 1:
                differences(i - 2)

        d_tiles = {}
        last_tile = NCH * TPC - 1
        back_banks = {}
        back_tags = ("t0", "t1", "t2", "m0", "m1")

        def turn_back(c):
            for h in range(2):
                bank = psum.tile([P, HALF * K], F32, name="lb%d_%d" % (c, h), tag=back_tags[(2 * c + h) % len(back_tags)])
                for s in range(HALF):
                    j = h * HALF + s
                    nc.tensor.transpose(bank[:, s * K : (s + 1) * K], l_tiles[c][:, j * P : (j + 1) * P], ident[:])
                back_banks[c, h] = bank

        def exps(c):
            dt_ = stream.tile([P, TPC * K], F32, name="dist%d" % c, tag="dist", bufs=6)
            d_tiles[c] = dt_
            if c in ROW_SUMS_ON_VECTOR:
                for h in range(2):
                    nc.scalar.activation(
                        out=dt_[:, h * HALF * K : (h + 1) * HALF * K], in_=back_banks[c, h][:], func=ACT.Exp, scale=-1.0
                    )
                return
            for j in range(TPC):
                t = c * TPC + j
                h, s = divmod(j, HALF)
                nc.scalar.activation(
                    out=dt_[:, j * K : (j + 1) * K],
                    in_=back_banks[c, h][:, s * K : (s + 1) * K],
                    func=ACT.Exp,
                    scale=-1.0,
                    accum_out=rsum[:, t : t + 1],
                )

        def memberships(c):
            dt_ = d_tiles[c]
            if c in ROW_SUMS_ON_VECTOR:
                nc.vector.tensor_reduce(
                    out=rsum[:, c * TPC : (c + 1) * TPC],
                    in_=dt_[:].rearrange("p (j k) -> p j k", j=TPC),
                    axis=mybir.AxisListType.X,
                    op=ALU.add,
                )
            halves = 2 if c == NCH - 1 else 1
            step = TPC // halves
            for h in range(halves):
                lo = c * TPC + h * step
                nc.vector.reciprocal(out=rrec[:, lo : lo + step], in_=rsum[:, lo : lo + step])
                for j in range(h * step, (h + 1) * step):
                    t = c * TPC + j
                    nc.vector.tensor_scalar_mul(
                        out=dt_[:, j * K : (j + 1) * K], in0=dt_[:, j * K : (j + 1) * K], scalar1=rrec[:, t : t + 1]
                    )
            nc.sync.dma_start(
                out=out_1[c * CHUNK : (c + 1) * CHUNK, :].rearrange("(p j) k -> p (j k)", j=TPC),
                in_=dt_[:],
            )

        facc_ps = psum.tile([P, P], F32, name="facc_ps", tag="t3")

        def column_sums(c):
            for j in range(TPC):
                t = c * TPC + j
                nc.tensor.matmul(
                    out=facc_ps[:],
                    lhsT=d_tiles[c][:, j * K : (j + 1) * K],
                    rhs=ident[:],
                    is_transpose=True,
                    start=(t == 0),
                    stop=(t == last_tile),
                )

        turn_back(0)
        for i in range(NCH + 2):
            if i + 1 < NCH:
                turn_back(i + 1)
            if i < NCH:
                exps(i)
            if 1 <= i <= NCH:
                memberships(i - 1)
            if 2 <= i:
                column_sums(i - 2)

        for n in range(3):
            spin(NCH - 1, "u0")

        ln_r = const.tile([P, P], F32, name="ln_r")
        acc_lnr = const.tile([P, 1], F32, name="acc_lnr")
        nc.scalar.activation(out=ln_r[:], in_=rsum[:], func=ACT.Ln, accum_out=acc_lnr[:])
        f_col = const.tile([P, 1], F32, name="f_col")
        nc.vector.tensor_reduce(out=f_col[:], in_=facc_ps[:], axis=mybir.AxisListType.X, op=ALU.add)
        lf_col = const.tile([P, 1], F32, name="lf_col")
        nc.scalar.activation(out=lf_col[:], in_=f_col[:], func=ACT.Ln)
        hlf = const.tile([P, P], F32, name="hlf")
        nc.vector.tensor_scalar_mul(out=hlf[:], in0=lf_col[:, 0:1].to_broadcast([P, P]), scalar1=0.5)

        x_tiles = {}
        m_banks = {}
        shifted_tiles = {}
        m_tags = ("t0", "t1", "m0", "m1")
        n_tags = ("t2", "u0", "u1", "t3")

        def shift(c):
            st = stream.tile([P, TPC * P], F32, name="shifted%d" % c, tag="shifted", bufs=5)
            shifted_tiles[c] = st
            if c < SHIFTS_ON_VECTOR:
                for h in range(2):
                    cols = slice(h * HALF * P, (h + 1) * HALF * P)
                    nc.vector.tensor_scalar_add(out=st[:, cols], in0=l_tiles[c][:, cols], scalar1=lf_col[:, 0:1])
                return
            nc.gpsimd.tensor_scalar(
                out=st[:], in0=l_tiles[c][:], scalar1=1.0, scalar2=lf_col[:, 0:1], op0=ALU.mult, op1=ALU.add
            )
            if c in BOTH_SHIFTS_ON_GPSIMD:
                nc.gpsimd.tensor_scalar(
                    out=l_tiles[c][:], in0=l_tiles[c][:], scalar1=1.0, scalar2=hlf[:, 0:1], op0=ALU.mult, op1=ALU.add
                )

        def sum_of_turns(bank, s, tiles):
            for n, part in enumerate(tiles):
                nc.tensor.matmul(
                    out=bank[:, s * K : (s + 1) * K],
                    lhsT=part,
                    rhs=ident[:],
                    is_transpose=True,
                    start=(n == 0),
                    stop=(n == len(tiles) - 1),
                )

        def turn_shifted(c):
            for h in range(2):
                index = (2 * c + h) % 4
                m_bank = psum.tile([P, HALF * K], F32, name="mm%d_%d" % (c, h), tag=m_tags[index])
                n_bank = psum.tile([P, HALF * K], F32, name="mn%d_%d" % (c, h), tag=n_tags[index])
                for s in range(HALF):
                    cols = slice((h * HALF + s) * P, (h * HALF + s + 1) * P)
                    sum_of_turns(m_bank, s, [l_tiles[c][:, cols]] if c in BOTH_SHIFTS_ON_GPSIMD else [l_tiles[c][:, cols], hlf[:]])
                for s in range(HALF):
                    cols = slice((h * HALF + s) * P, (h * HALF + s + 1) * P)
                    sum_of_turns(n_bank, s, [shifted_tiles[c][:, cols]])
                m_banks[c, h] = (m_bank, n_bank)

        def weights(c):
            xt_ = stream.tile([P, TPC * K], F32, name="x%d" % c, tag="x", bufs=3)
            x_tiles[c] = xt_
            for j in range(TPC):
                t = c * TPC + j
                h, s = divmod(j, HALF)
                nc.scalar.activation(
                    out=xt_[:, j * K : (j + 1) * K],
                    in_=m_banks[c, h][0][:, s * K : (s + 1) * K],
                    func=ACT.Exp,
                    scale=-2.0,
                    accum_out=ssum[:, t : t + 1],
                )

        y_junk = const.tile([P, 4 * K], F32, name="y_junk")

        def sums(c):
            for j in range(TPC):
                t = c * TPC + j
                h, s = divmod(j, HALF)
                nc.vector.scalar_tensor_tensor(
                    out=y_junk[:, s * K : (s + 1) * K],
                    in0=m_banks[c, h][1][:, s * K : (s + 1) * K],
                    scalar=1.0,
                    in1=x_tiles[c][:, j * K : (j + 1) * K],
                    op0=ALU.mult,
                    op1=ALU.mult,
                    accum_out=tsum[:, t : t + 1],
                )
            if c in RECIPROCALS_AFTER:
                first = max([0] + [x + 1 for x in RECIPROCALS_AFTER if x < c])
                cols = slice(first * TPC, (c + 1) * TPC)
                nc.vector.reciprocal(out=srec[:, cols], in_=ssum[:, cols])

        def weighted(first, last, n):
            cols = slice(first * TPC, (last + 1) * TPC)
            nc.vector.scalar_tensor_tensor(
                out=diag_junk[:, cols],
                in0=tsum[:, cols],
                scalar=1.0,
                in1=srec[:, cols],
                op0=ALU.mult,
                op1=ALU.mult,
                accum_out=acc_t[n][:],
            )

        acc_t = [const.tile([P, 1], F32, name="acc_t%d" % n) for n in range(2)]
        for c in range(4):
            shift(c)
        for c in range(NCH + 1):
            if c < NCH:
                turn_shifted(c)
                weights(c)
            if c + 4 < NCH:
                shift(c + 4)
            if 1 <= c:
                if c == NCH:
                    weighted(0, NCH - 3, 0)
                sums(c - 1)

        ln_s = const.tile([P, P], F32, name="ln_s")
        acc_lns = const.tile([P, 1], F32, name="acc_lns")
        nc.scalar.activation(out=ln_s[:], in_=ssum[:], func=ACT.Ln, accum_out=acc_lns[:])
        weighted(NCH - 2, NCH - 1, 1)
        tot_ps = psum.tile([P, 1], F32, name="tot_ps", tag="t0")
        terms = ((mean_plus, acc_lnr), (mean_minus, acc_t[0]), (mean_minus, acc_lns), (mean_minus, acc_t[1]))
        for n, (factor, column) in enumerate(terms):
            nc.tensor.matmul(out=tot_ps[:], lhsT=factor[:], rhs=column[:], start=(n == 0), stop=(n == len(terms) - 1))
        res = const.tile([P, 1], F32, name="res")
        nc.scalar.copy(out=res[:], in_=tot_ps[:])
        loss_ap = out_0
        for extra in range(2 - len(out_0.shape)):
            loss_ap = loss_ap.unsqueeze(0)
        nc.sync.dma_start(out=loss_ap, in_=res[0:1, 0:1])
